import numpy as np
import ml_dtypes


def mxq(x, axis, fmt="e4m3"):
    dtype, down = {"e4m3": (ml_dtypes.float8_e4m3fn, 7), "e5m2": (ml_dtypes.float8_e5m2, 14)}[fmt]
    v = np.moveaxis(np.asarray(x, np.float32).astype(ml_dtypes.bfloat16).astype(np.float64), axis, -1)
    blocks = v.reshape(v.shape[:-1] + (-1, 32))
    amax = np.abs(blocks).max(-1, keepdims=True)
    byte = np.maximum(np.where(amax > 0, np.frexp(amax)[1] - 1 + 127, 0) - down, 1)
    scale = np.exp2(byte - 127.0)
    codes = (blocks / scale).astype(np.float32).astype(dtype).astype(np.float64)
    return np.moveaxis((codes * scale).reshape(v.shape), -1, axis)


WIDE = False


def mx_kscale(k):
    if not WIDE:
        return np.ones(k)
    levels = np.array([10, -10, 5, -5, 0])
    a = np.random.permutation(np.resize(levels, k // 512 * 4)).reshape(k // 512, 4)
    idx = np.arange(k)
    return np.exp2(a[idx // 512, idx % 128 // 32])


BF16 = ml_dtypes.bfloat16


def bf(x):
    return np.asarray(x, np.float32).astype(BF16)


def f64(x):
    return np.asarray(x).astype(np.float64)


E2M1 = np.array([0.0, 0.5, 1.0, 1.5, 2.0, 3.0, 4.0, 6.0, -0.0, -0.5, -1.0, -1.5, -2.0, -3.0, -4.0, -6.0])


def pack_weight(w, fmt):
    k, n = w.shape
    w = f64(bf(w)).reshape(k // 32, 32, n)
    amax = np.abs(w).max(1)
    if fmt == "e4m3":
        byte = np.frexp(amax)[1] - 1 + 127 - 7
    else:
        mant, ex = np.frexp(amax / 6.0)
        byte = np.where(mant > 0.5, ex, ex - 1) + 127
    byte = np.clip(np.where(amax > 0, byte, 1), 1, 254)
    scaled = (w * np.exp2(127.0 - byte)[:, None, :]).reshape(k, n).astype(np.float32)
    by_word = np.ascontiguousarray(scaled.reshape(k // 512, 128, 4, n).transpose(0, 1, 3, 2))
    if fmt == "e4m3":
        words = by_word.astype(ml_dtypes.float8_e4m3fn).view(np.uint8)
    else:
        c = by_word.astype(ml_dtypes.float4_e2m1fn).view(np.uint8) & 0xF
        words = c[..., 0::2] | (c[..., 1::2] << 4)
    return np.ascontiguousarray(words), np.ascontiguousarray(byte.astype(np.uint8).reshape(k // 512, 16, n))


def unpack_weight(words, scales, fmt):
    g, p, n, _ = words.shape
    if fmt == "e4m3":
        vals = np.ascontiguousarray(words).view(ml_dtypes.float8_e4m3fn).astype(np.float64)
    else:
        nib = np.empty((g, p, n, 4), np.uint8)
        nib[..., 0::2] = words & 0xF
        nib[..., 1::2] = words >> 4
        vals = E2M1[nib]
    vals = vals * np.repeat(np.exp2(scales.astype(np.float64) - 127.0), 8, axis=1)[..., None]
    return vals.transpose(0, 1, 3, 2).reshape(g * 512, n)


B, E, D, H = 256, 8, 128, 1024
FACTOR = 1.0


def swish(v):
    return v / (1.0 + np.exp(-v))


def setup_inputs():
    s = mx_kscale(H)
    h2 = bf(swish(np.random.standard_normal((B, E, H)) * 1.5) * s)
    w3 = np.random.standard_normal((E, H, H)) * 1.5 / np.sqrt(H) / s[:, None]
    W3_words, W3_scales = pack_weight(w3.reshape(-1, H), "e4m3")
    b3 = bf(np.random.standard_normal((E, H)) * 0.3)
    w4 = np.random.standard_normal((E, H, D)) / np.sqrt(H)
    W4_words, W4_scales = pack_weight(w4.reshape(-1, D), "e4m3")
    b4 = bf(np.random.standard_normal((E, D)) * 0.3)
    return {"h2": h2,
            "W3_words": W3_words,
            "W3_scales": W3_scales,
            "b3": b3,
            "W4_words": W4_words,
            "W4_scales": W4_scales,
            "b4": b4}


def reference(h2, W3_words, W3_scales, b3, W4_words, W4_scales, b4):
    x = f64(h2).transpose(1, 0, 2)
    h3 = swish((mxq(x, 2, "e4m3") @ unpack_weight(W3_words, W3_scales, "e4m3").reshape(E, H, H)) + f64(b3)[:, None, :])
    out = ((mxq(h3, 2, "e4m3") @ unpack_weight(W4_words, W4_scales, "e4m3").reshape(E, H, D)) + f64(b4)[:, None, :]) * FACTOR
    return out.transpose(1, 0, 2).reshape(-1, D)

@@ -1,0 +1,273 @@
+from contextlib import ExitStack
+
+import concourse.mybir as mybir
+from concourse.masks import make_identity
+
+F32 = mybir.dt.float32
+BF16 = mybir.dt.bfloat16
+U8 = mybir.dt.uint8
+U32 = mybir.dt.uint32
+I32 = mybir.dt.int32
+FP8X4 = mybir.dt.float8_e4m3fn_x4
+SILU = mybir.ActivationFunctionType.Silu
+ADD = mybir.AluOpType.add
+
+B, E, H, D = 256, 8, 1024, 128
+P = 128
+PACK = 4
+K_PASS = P * PACK
+PASSES = H // K_PASS
+HALVES = B // P
+N_TILE = 512
+N_TILES = H // N_TILE
+PLANES = 4
+QUADS = 4
+PAIR_WORDS = 2
+
+FLOPS = 2 * B * E * H * (H + D)
+
+
+def tile_environvectorfield_pb_e_kernel(
+    tc, h2, W3_words, W3_scales, b3, W4_words, W4_scales, b4, out
+):
+    nc = tc.nc
+    with ExitStack() as ctx:
+        const = ctx.enter_context(tc.tile_pool(name="const", bufs=1))
+        h2_pool = ctx.enter_context(tc.tile_pool(name="h2", bufs=E))
+        w3_pool = ctx.enter_context(tc.tile_pool(name="w3", bufs=E))
+        work = ctx.enter_context(tc.tile_pool(name="work", bufs=2))
+        psum_mx = ctx.enter_context(tc.psum_pool(name="psum_mx", bufs=4))
+        psum_tr = ctx.enter_context(tc.psum_pool(name="psum_tr", bufs=4))
+        ctx.enter_context(tc.manual_schedule())
+
+        h2_by_env = h2.rearrange("(p i) e k -> p i e k", i=HALVES)
+        out_by_env = out.rearrange("(p i e) d -> p i e d", i=HALVES, e=E)
+        w3_words_dram = W3_words.rearrange("g p n t -> g p (n t)").bitcast(I32)
+        w4_words_dram = W4_words.rearrange("g p n t -> g p (n t)").bitcast(I32)
+        w3_scales_dram = W3_scales.bitcast(I32)
+        w4_scales_dram = W4_scales.bitcast(I32)
+
+        w3_planes = const.tile([P, E * PASSES // PLANES, H], U8, align_bytes=64)
+        w4_planes = const.tile([P, E * PASSES, D], U8, align_bytes=64)
+        w4_sb = const.tile([P, E * PASSES, D], U32, align_bytes=64)
+        b3_rows = const.tile([P, K_PASS], BF16)
+        b4_row = const.tile([P, E * D], BF16)
+        ones = const.tile([P, P], BF16)
+        ident = const.tile([P, P], F32)
+        out_sb = const.tile([P, HALVES, E, D], F32)
+
+        nc.vector.memset(w3_planes[:].rearrange("p a n -> p (a n)").bitcast(I32), 0)
+        nc.vector.memset(b3_rows[:], 0.0)
+        nc.vector.memset(b4_row[:], 0.0)
+        nc.vector.memset(w4_planes[:].rearrange("p g d -> p (g d)").bitcast(I32), 0)
+        nc.vector.memset(ones[:], 1.0)
+        make_identity(nc, ident[:])
+
+        h2_tiles = {}
+        w3_tiles = {}
+
+        def load_h2(e):
+            h2_sb = h2_pool.tile([P, HALVES, H], BF16)
+            nc.sync.dma_start(out=h2_sb[:], in_=h2_by_env[:, :, e, :])
+            h2_tiles[e] = h2_sb
+
+        def load_w3(e):
+            w3_sb = w3_pool.tile([P, PASSES, H], U32, align_bytes=64)
+            for g in range(PASSES):
+                nc.sync.dma_start(
+                    out=w3_sb[:, g, :].bitcast(I32), in_=w3_words_dram[PASSES * e + g]
+                )
+            w3_tiles[e] = w3_sb
+
+        def load_w3_planes(a):
+            for quad in range(QUADS):
+                nc.sync.dma_start(
+                    out=w3_planes[32 * quad : 32 * quad + 16, a, :].bitcast(I32),
+                    in_=w3_scales_dram[PLANES * a : PLANES * (a + 1), 4 * quad : 4 * quad + 4, :],
+                )
+
+        def load_w4_planes():
+            for quad in range(QUADS):
+                nc.sync.dma_start(
+                    out=w4_planes[32 * quad : 32 * quad + 4, :, :].bitcast(I32),
+                    in_=w4_scales_dram[:, 4 * quad : 4 * quad + 4, :].rearrange("g r d -> r g d"),
+                )
+
+        def load_w4(a):
+            passes = slice(PLANES * a, PLANES * (a + 1))
+            nc.sync.dma_start(
+                out=w4_sb[:, passes, :].bitcast(I32),
+                in_=w4_words_dram[passes].rearrange("g p n -> p g n"),
+            )
+
+        load_h2(0)
+        nc.sync.dma_start(out=b3_rows[0 : E * PASSES, :], in_=b3.rearrange("e (h n) -> (e h) n", h=N_TILES))
+        nc.sync.dma_start(out=b4_row[0:1, :], in_=b4.rearrange("(o e) d -> o (e d)", o=1))
+        load_w3_planes(0)
+        load_w3(0)
+        load_h2(1)
+        load_w4_planes()
+        load_w4(0)
+        load_w3(1)
+        for a in range(1, E // 2):
+            load_h2(2 * a)
+            load_w3_planes(a)
+            load_w4(a)
+            load_w3(2 * a)
+            load_h2(2 * a + 1)
+            load_w3(2 * a + 1)
+
+        def copy_out(i, dst, src):
+            if i == 0:
+                nc.vector.tensor_copy(out=dst, in_=src)
+            else:
+                nc.scalar.copy(out=dst, in_=src)
+
+        x_grouped_tiles = {}
+        x_mx = {}
+        z_tiles = {}
+        h3_plane_tiles = {}
+        h3_grouped_tiles = {}
+        h3_mx = {}
+
+        def transpose_x(e):
+            x_grouped = work.tile([P, PASSES * HALVES * P * PACK], BF16, align_bytes=64)
+            grouped_pairs = x_grouped[:].bitcast(F32).rearrange(
+                "p (g i b u) -> p g i b u", g=PASSES, i=HALVES, b=P
+            )
+            words_in_pass = K_PASS // 2
+            for i in range(HALVES):
+                x_pairs = h2_tiles[e][:, i, :].bitcast(F32)
+                xt = psum_tr.tile([P, PASSES, PAIR_WORDS, P], F32, tag="tr")
+                for g in range(PASSES):
+                    for u in range(PAIR_WORDS):
+                        nc.tensor.transpose(
+                            out=xt[:, g, u, :],
+                            in_=x_pairs[:, words_in_pass * g + u : words_in_pass * (g + 1) : PAIR_WORDS],
+                            identity=ident[:],
+                        )
+                copy_out(i, grouped_pairs[:, :, i, :, :], xt[:].rearrange("p g u b -> p g b u"))
+            x_grouped_tiles[e] = x_grouped
+
+        def quantise(grouped, label):
+            words = work.tile([P, PASSES, HALVES, P], U32, align_bytes=64, tag=label + "_words")
+            scales = work.tile([P, PASSES, HALVES, P], U8, align_bytes=64, tag=label + "_scales")
+            nc.vector.quantize_mx(
+                out=words[:].rearrange("p g i b -> p (g i b)").bitcast(FP8X4),
+                scales=scales[:].rearrange("p g i b -> p (g i b)"),
+                in_=grouped[:],
+            )
+            return words, scales
+
+        def regroup_h3(e, h):
+            if h == 0:
+                h3_grouped = work.tile([P, PASSES * B * PACK], BF16, align_bytes=64)
+                h3_grouped_tiles[e] = h3_grouped
+            grouped = h3_grouped_tiles[e][:].rearrange("p (h b t) -> p h b t", h=PASSES, t=PACK)
+            nc.vector.tensor_copy(
+                out=grouped[:, h, :, :].rearrange("p (c j) t -> p c t j", j=4),
+                in_=h3_plane_tiles[e][:, h, :, :].rearrange("p t (c j) -> p c t j", j=4),
+            )
+
+        def stage1(e):
+            words, scales = x_mx[e]
+            z = work.tile([P, HALVES, N_TILES, PACK, P], F32)
+            for h in range(N_TILES):
+                cols = slice(N_TILE * h, N_TILE * (h + 1))
+                for i in range(HALVES):
+                    acc = psum_mx.tile([P, N_TILE], F32, tag="mx")
+                    for g in range(PASSES):
+                        a, c = divmod(PASSES * e + g, PLANES)
+                        nc.tensor.matmul_mx(
+                            out=acc[:],
+                            lhsT=words[:, g, i, :].bitcast(FP8X4),
+                            lhsT_scale=scales[:, g, i, :],
+                            rhs=w3_tiles[e][:, g, cols].bitcast(FP8X4),
+                            rhs_scale=w3_planes[4 * c : P, a, cols],
+                            start=(g == 0),
+                            stop=(g == PASSES - 1),
+                        )
+                    copy_out(i, z[:, i, h, :, :], acc[:].rearrange("b (p t) -> b t p", t=PACK))
+                if e > 0:
+                    regroup_h3(e - 1, h)
+            z_tiles[e] = z
+
+        def transpose_h3(e):
+            h3_planes = work.tile([P, PASSES, PACK, B], BF16)
+            for h in range(PASSES):
+                for first_t in range(0, PACK, 2):
+                    ht = psum_tr.tile([P, 2, HALVES, P], F32, tag="tr")
+                    for j in range(2):
+                        for i in range(HALVES):
+                            nc.tensor.transpose(
+                                out=ht[:, j, i, :],
+                                in_=z_tiles[e][:, i, h, first_t + j, :],
+                                identity=ident[:],
+                            )
+                    for j in range(2):
+                        t = first_t + j
+                        nc.scalar.activation(
+                            out=h3_planes[:, h, t, :],
+                            in_=ht[:, j, :, :].rearrange("p i b -> p (i b)"),
+                            func=SILU,
+                            bias=b3_cols[:, PASSES * e + h, t : t + 1],
+                            scale=1.0,
+                        )
+            h3_plane_tiles[e] = h3_planes
+
+        def stage2(e):
+            words, scales = h3_mx[e]
+            o = psum_mx.tile([P, HALVES, D], F32, tag="mx")
+            for i in range(HALVES):
+                for h in range(PASSES):
+                    nc.tensor.matmul_mx(
+                        out=o[:, i, :],
+                        lhsT=words[:, h, i, :].bitcast(FP8X4),
+                        lhsT_scale=scales[:, h, i, :],
+                        rhs=w4_sb[:, PASSES * e + h, :].bitcast(FP8X4),
+                        rhs_scale=w4_planes[:, PASSES * e + h, :],
+                        start=(h == 0),
+                        stop=(h == PASSES - 1),
+                    )
+            nc.vector.tensor_tensor(
+                out=out_sb[:, :, e, :],
+                in0=o[:],
+                in1=b4_all[:, e, :].unsqueeze(1).to_broadcast([P, HALVES, D]),
+                op=ADD,
+            )
+            nc.sync.dma_start(out=out_by_env[:, :, e, :], in_=out_sb[:, :, e, :])
+
+        transpose_x(0)
+
+        b3_sorted = const.tile([P, PACK, P], F32)
+        nc.vector.tensor_copy(out=b3_sorted[:], in_=b3_rows[:].rearrange("r (p t) -> r t p", t=PACK))
+        x_mx[0] = quantise(x_grouped_tiles[0], "x")
+        b3_t = psum_tr.tile([P, PACK, P], F32, tag="tr")
+        for t in range(PACK):
+            nc.tensor.transpose(out=b3_t[:, t, :], in_=b3_sorted[:, t, :], identity=ident[:])
+        b3_cols = const.tile([P, E * PASSES, PACK], F32)
+        nc.vector.tensor_copy(
+            out=b3_cols[:], in_=b3_t[:, :, 0 : E * PASSES].rearrange("p t r -> p r t")
+        )
+        b4_all = const.tile([P, E, D], F32)
+        for c in range(E * D // N_TILE):
+            b4_bank = psum_tr.tile([P, N_TILE], F32, tag="tr")
+            cols = slice(N_TILE * c, N_TILE * (c + 1))
+            nc.tensor.matmul(out=b4_bank[:], lhsT=ones[:], rhs=b4_row[:, cols], start=True, stop=True)
+            nc.scalar.copy(out=b4_all[:].rearrange("p e d -> p (e d)")[:, cols], in_=b4_bank[:])
+
+        for e in range(E):
+            stage1(e)
+            if e + 1 < E:
+                transpose_x(e + 1)
+            if e > 0:
+                h3_mx[e - 1] = quantise(h3_grouped_tiles[e - 1], "h3")
+            transpose_h3(e)
+            if e + 1 < E:
+                x_mx[e + 1] = quantise(x_grouped_tiles[e + 1], "x")
+            if e > 0:
+                stage2(e - 1)
+        for h in range(PASSES):
+            regroup_h3(E - 1, h)
+        h3_mx[E - 1] = quantise(h3_grouped_tiles[E - 1], "h3")
+        stage2(E - 1)

@@ -18,8 +18,8 @@ PACK = 4
 K_PASS = P * PACK
 PASSES = H // K_PASS
 HALVES = B // P
-N_TILE = 512
-N_TILES = H // N_TILE
+BANK = 512
+PAIRS = 2
 PLANES = 4
 QUADS = 4
 PAIR_WORDS = 2
@@ -37,7 +37,8 @@ def tile_environvectorfield_pb_e_kernel(
         w3_pool = ctx.enter_context(tc.tile_pool(name="w3", bufs=E))
         work = ctx.enter_context(tc.tile_pool(name="work", bufs=2))
         psum_mx = ctx.enter_context(tc.psum_pool(name="psum_mx", bufs=4))
-        psum_tr = ctx.enter_context(tc.psum_pool(name="psum_tr", bufs=4))
+        psum_tr = ctx.enter_context(tc.psum_pool(name="psum_tr", bufs=2))
+        psum_o = ctx.enter_context(tc.psum_pool(name="psum_o", bufs=2))
         ctx.enter_context(tc.manual_schedule())
 
         h2_by_env = h2.rearrange("(p i) e k -> p i e k", i=HALVES)
@@ -48,6 +49,7 @@ def tile_environvectorfield_pb_e_kernel(
         w4_scales_dram = W4_scales.bitcast(I32)
 
         w3_planes = const.tile([P, E * PASSES // PLANES, H], U8, align_bytes=64)
+        w3_planes_perm = const.tile([P, E * PASSES // PLANES, H], U8, align_bytes=64)
         w4_planes = const.tile([P, E * PASSES, D], U8, align_bytes=64)
         w4_sb = const.tile([P, E * PASSES, D], U32, align_bytes=64)
         b3_rows = const.tile([P, K_PASS], BF16)
@@ -101,7 +103,9 @@ def tile_environvectorfield_pb_e_kernel(
             )
 
         load_h2(0)
-        nc.sync.dma_start(out=b3_rows[0 : E * PASSES, :], in_=b3.rearrange("e (h n) -> (e h) n", h=N_TILES))
+        nc.sync.dma_start(
+            out=b3_rows[0 : E * PASSES, :], in_=b3.rearrange("e (h n) -> (e h) n", h=PASSES)
+        )
         nc.sync.dma_start(out=b4_row[0:1, :], in_=b4.rearrange("(o e) d -> o (e d)", o=1))
         load_w3_planes(0)
         load_w3(0)
@@ -117,20 +121,14 @@ def tile_environvectorfield_pb_e_kernel(
             load_h2(2 * a + 1)
             load_w3(2 * a + 1)
 
-        def copy_out(i, dst, src):
-            if i == 0:
-                nc.vector.tensor_copy(out=dst, in_=src)
-            else:
-                nc.scalar.copy(out=dst, in_=src)
-
         x_grouped_tiles = {}
         x_mx = {}
-        z_tiles = {}
+        w3_perm_tiles = {}
         h3_plane_tiles = {}
         h3_grouped_tiles = {}
         h3_mx = {}
 
-        def transpose_x(e):
+        def transpose_x(e, first_half_on_vector=False):
             x_grouped = work.tile([P, PASSES * HALVES * P * PACK], BF16, align_bytes=64)
             grouped_pairs = x_grouped[:].bitcast(F32).rearrange(
                 "p (g i b u) -> p g i b u", g=PASSES, i=HALVES, b=P
@@ -146,7 +144,12 @@ def tile_environvectorfield_pb_e_kernel(
                             in_=x_pairs[:, words_in_pass * g + u : words_in_pass * (g + 1) : PAIR_WORDS],
                             identity=ident[:],
                         )
-                copy_out(i, grouped_pairs[:, :, i, :, :], xt[:].rearrange("p g u b -> p g b u"))
+                dst = grouped_pairs[:, :, i, :, :]
+                src = xt[:].rearrange("p g u b -> p g b u")
+                if first_half_on_vector and i == 0:
+                    nc.vector.tensor_copy(out=dst, in_=src)
+                else:
+                    nc.scalar.copy(out=dst, in_=src)
             x_grouped_tiles[e] = x_grouped
 
         def quantise(grouped, label):
@@ -159,6 +162,55 @@ def tile_environvectorfield_pb_e_kernel(
             )
             return words, scales
 
+        def permute_w3_planes(a):
+            nc.vector.tensor_copy(
+                out=w3_planes_perm[:, a, :].rearrange("p (h t m) -> p h t m", h=PASSES, t=PACK),
+                in_=w3_planes[:, a, :].rearrange("p (h m t) -> p h t m", h=PASSES, t=PACK),
+            )
+
+        def permute_w3(e):
+            w3_perm = work.tile([P, PASSES, PASSES, PACK, P], U32, align_bytes=64)
+            for g in range(PASSES):
+                nc.vector.tensor_copy(
+                    out=w3_perm[:, g, :, :, :].bitcast(I32),
+                    in_=w3_tiles[e][:, g, :]
+                    .bitcast(I32)
+                    .rearrange("p (h m t) -> p h t m", h=PASSES, t=PACK),
+                )
+            w3_perm_tiles[e] = w3_perm
+
+        def stage1(e, h):
+            words, scales = x_mx[e]
+            if h == 0:
+                h3_planes = work.tile([P, PASSES, PACK, B], BF16)
+                h3_plane_tiles[e] = h3_planes
+            planes = h3_plane_tiles[e]
+            for pair in range(PAIRS):
+                acc = psum_mx.tile([P, PACK // PAIRS, B], F32, tag="mx")
+                for j in range(PACK // PAIRS):
+                    t = pair * (PACK // PAIRS) + j
+                    cols = slice(K_PASS * h + P * t, K_PASS * h + P * (t + 1))
+                    for g in range(PASSES):
+                        a, c = divmod(PASSES * e + g, PLANES)
+                        nc.tensor.matmul_mx(
+                            out=acc[:, j, :],
+                            lhsT=w3_perm_tiles[e][:, g, h, t, :].bitcast(FP8X4),
+                            lhsT_scale=w3_planes_perm[4 * c : P, a, cols],
+                            rhs=words[:, g, :, :].rearrange("p i b -> p (i b)").bitcast(FP8X4),
+                            rhs_scale=scales[:, g, :, :].rearrange("p i b -> p (i b)"),
+                            start=(g == 0),
+                            stop=(g == PASSES - 1),
+                        )
+                for j in range(PACK // PAIRS):
+                    t = pair * (PACK // PAIRS) + j
+                    nc.scalar.activation(
+                        out=planes[:, h, t, :],
+                        in_=acc[:, j, :],
+                        func=SILU,
+                        bias=b3_cols[:, PASSES * e + h, t : t + 1],
+                        scale=1.0,
+                    )
+
         def regroup_h3(e, h):
             if h == 0:
                 h3_grouped = work.tile([P, PASSES * B * PACK], BF16, align_bytes=64)
@@ -169,55 +221,9 @@ def tile_environvectorfield_pb_e_kernel(
                 in_=h3_plane_tiles[e][:, h, :, :].rearrange("p t (c j) -> p c t j", j=4),
             )
 
-        def stage1(e):
-            words, scales = x_mx[e]
-            z = work.tile([P, HALVES, N_TILES, PACK, P], F32)
-            for h in range(N_TILES):
-                cols = slice(N_TILE * h, N_TILE * (h + 1))
-                for i in range(HALVES):
-                    acc = psum_mx.tile([P, N_TILE], F32, tag="mx")
-                    for g in range(PASSES):
-                        a, c = divmod(PASSES * e + g, PLANES)
-                        nc.tensor.matmul_mx(
-                            out=acc[:],
-                            lhsT=words[:, g, i, :].bitcast(FP8X4),
-                            lhsT_scale=scales[:, g, i, :],
-                            rhs=w3_tiles[e][:, g, cols].bitcast(FP8X4),
-                            rhs_scale=w3_planes[4 * c : P, a, cols],
-                            start=(g == 0),
-                            stop=(g == PASSES - 1),
-                        )
-                    copy_out(i, z[:, i, h, :, :], acc[:].rearrange("b (p t) -> b t p", t=PACK))
-                if e > 0:
-                    regroup_h3(e - 1, h)
-            z_tiles[e] = z
-
-        def transpose_h3(e):
-            h3_planes = work.tile([P, PASSES, PACK, B], BF16)
-            for h in range(PASSES):
-                for first_t in range(0, PACK, 2):
-                    ht = psum_tr.tile([P, 2, HALVES, P], F32, tag="tr")
-                    for j in range(2):
-                        for i in range(HALVES):
-                            nc.tensor.transpose(
-                                out=ht[:, j, i, :],
-                                in_=z_tiles[e][:, i, h, first_t + j, :],
-                                identity=ident[:],
-                            )
-                    for j in range(2):
-                        t = first_t + j
-                        nc.scalar.activation(
-                            out=h3_planes[:, h, t, :],
-                            in_=ht[:, j, :, :].rearrange("p i b -> p (i b)"),
-                            func=SILU,
-                            bias=b3_cols[:, PASSES * e + h, t : t + 1],
-                            scale=1.0,
-                        )
-            h3_plane_tiles[e] = h3_planes
-
         def stage2(e):
             words, scales = h3_mx[e]
-            o = psum_mx.tile([P, HALVES, D], F32, tag="mx")
+            o = psum_o.tile([P, HALVES, D], F32, tag="o")
             for i in range(HALVES):
                 for h in range(PASSES):
                     nc.tensor.matmul_mx(
@@ -237,11 +243,12 @@ def tile_environvectorfield_pb_e_kernel(
             )
             nc.sync.dma_start(out=out_by_env[:, :, e, :], in_=out_sb[:, :, e, :])
 
-        transpose_x(0)
+        transpose_x(0, first_half_on_vector=True)
 
         b3_sorted = const.tile([P, PACK, P], F32)
         nc.vector.tensor_copy(out=b3_sorted[:], in_=b3_rows[:].rearrange("r (p t) -> r t p", t=PACK))
         x_mx[0] = quantise(x_grouped_tiles[0], "x")
+        permute_w3_planes(0)
         b3_t = psum_tr.tile([P, PACK, P], F32, tag="tr")
         for t in range(PACK):
             nc.tensor.transpose(out=b3_t[:, t, :], in_=b3_sorted[:, t, :], identity=ident[:])
@@ -250,23 +257,32 @@ def tile_environvectorfield_pb_e_kernel(
             out=b3_cols[:], in_=b3_t[:, :, 0 : E * PASSES].rearrange("p t r -> p r t")
         )
         b4_all = const.tile([P, E, D], F32)
-        for c in range(E * D // N_TILE):
-            b4_bank = psum_tr.tile([P, N_TILE], F32, tag="tr")
-            cols = slice(N_TILE * c, N_TILE * (c + 1))
+        for c in range(E * D // BANK):
+            b4_bank = psum_tr.tile([P, BANK], F32, tag="tr")
+            cols = slice(BANK * c, BANK * (c + 1))
             nc.tensor.matmul(out=b4_bank[:], lhsT=ones[:], rhs=b4_row[:, cols], start=True, stop=True)
             nc.scalar.copy(out=b4_all[:].rearrange("p e d -> p (e d)")[:, cols], in_=b4_bank[:])
+        permute_w3(0)
+        transpose_x(1)
 
         for e in range(E):
-            stage1(e)
-            if e + 1 < E:
-                transpose_x(e + 1)
+            stage1(e, 0)
             if e > 0:
-                h3_mx[e - 1] = quantise(h3_grouped_tiles[e - 1], "h3")
-            transpose_h3(e)
+                for h in range(PASSES):
+                    regroup_h3(e - 1, h)
             if e + 1 < E:
                 x_mx[e + 1] = quantise(x_grouped_tiles[e + 1], "x")
             if e > 0:
+                h3_mx[e - 1] = quantise(h3_grouped_tiles[e - 1], "h3")
+            if e + 1 < E:
+                if (e + 1) % 2 == 0:
+                    permute_w3_planes((e + 1) // 2)
+                permute_w3(e + 1)
+            stage1(e, 1)
+            if e > 0:
                 stage2(e - 1)
+            if e + 2 < E:
+                transpose_x(e + 2)
         for h in range(PASSES):
             regroup_h3(E - 1, h)
         h3_mx[E - 1] = quantise(h3_grouped_tiles[E - 1], "h3")

@@ -164,19 +164,26 @@ def tile_environvectorfield_pb_e_kernel(
 
         def permute_w3_planes(a):
             nc.vector.tensor_copy(
-                out=w3_planes_perm[:, a, :].rearrange("p (h t m) -> p h t m", h=PASSES, t=PACK),
-                in_=w3_planes[:, a, :].rearrange("p (h m t) -> p h t m", h=PASSES, t=PACK),
+                out=w3_planes_perm[:, a, :].rearrange(
+                    "p (h t c j) -> p h c t j", h=PASSES, t=PACK, j=16
+                ),
+                in_=w3_planes[:, a, :].rearrange(
+                    "p (h c j t) -> p h c t j", h=PASSES, t=PACK, j=16
+                ),
             )
 
         def permute_w3(e):
             w3_perm = work.tile([P, PASSES, PASSES, PACK, P], U32, align_bytes=64)
             for g in range(PASSES):
-                nc.vector.tensor_copy(
-                    out=w3_perm[:, g, :, :, :].bitcast(I32),
-                    in_=w3_tiles[e][:, g, :]
-                    .bitcast(I32)
-                    .rearrange("p (h m t) -> p h t m", h=PASSES, t=PACK),
-                )
+                for h in range(PASSES):
+                    nc.vector.tensor_copy(
+                        out=w3_perm[:, g, h, :, :]
+                        .bitcast(I32)
+                        .rearrange("p t (c j) -> p c t j", j=4),
+                        in_=w3_tiles[e][:, g, K_PASS * h : K_PASS * (h + 1)]
+                        .bitcast(I32)
+                        .rearrange("p (c j t) -> p c t j", j=4, t=PACK),
+                    )
             w3_perm_tiles[e] = w3_perm
 
         def stage1(e, h):

@@ -58,26 +58,37 @@ def tile_environvectorfield_pb_e_kernel(
         ident = const.tile([P, P], F32)
         out_sb = const.tile([P, HALVES, E, D], F32)
 
-        nc.vector.memset(w3_planes[:].rearrange("p a n -> p (a n)").bitcast(I32), 0)
+        warm_up = const.tile([P, 1], F32)
+        nc.vector.memset(warm_up[:], 0.0)
+        nc.scalar.activation(out=warm_up[:], in_=warm_up[:], func=SILU, scale=1.0)
+        nc.vector.memset(w3_planes[:, 0, :].bitcast(I32), 0)
         nc.vector.memset(b3_rows[:], 0.0)
-        nc.vector.memset(b4_row[:], 0.0)
-        nc.vector.memset(w4_planes[:].rearrange("p g d -> p (g d)").bitcast(I32), 0)
-        nc.vector.memset(ones[:], 1.0)
         make_identity(nc, ident[:])
+        nc.vector.memset(
+            w3_planes[:, 1 : E * PASSES // PLANES, :].rearrange("p a n -> p (a n)").bitcast(I32), 0
+        )
+        nc.vector.memset(w4_planes[:].rearrange("p g d -> p (g d)").bitcast(I32), 0)
+        nc.vector.memset(b4_row[:], 0.0)
+        nc.vector.memset(ones[:], 1.0)
 
         h2_tiles = {}
         w3_tiles = {}
 
-        def load_h2(e):
+        def load_h2(e, pieces=1):
             h2_sb = h2_pool.tile([P, HALVES, H], BF16)
-            nc.sync.dma_start(out=h2_sb[:], in_=h2_by_env[:, :, e, :])
+            width = H // pieces
+            for n in range(pieces):
+                cols = slice(width * n, width * (n + 1))
+                nc.sync.dma_start(out=h2_sb[:, :, cols], in_=h2_by_env[:, :, e, cols])
             h2_tiles[e] = h2_sb
 
         def load_w3(e):
             w3_sb = w3_pool.tile([P, PASSES, H], U32, align_bytes=64)
-            for g in range(PASSES):
+            for h in range(PASSES):
+                cols = slice(K_PASS * h, K_PASS * (h + 1))
                 nc.sync.dma_start(
-                    out=w3_sb[:, g, :].bitcast(I32), in_=w3_words_dram[PASSES * e + g]
+                    out=w3_sb[:, :, cols].bitcast(I32),
+                    in_=w3_words_dram[PASSES * e : PASSES * (e + 1), :, cols].rearrange("g p n -> p g n"),
                 )
             w3_tiles[e] = w3_sb
 
@@ -102,17 +113,17 @@ def tile_environvectorfield_pb_e_kernel(
                 in_=w4_words_dram[passes].rearrange("g p n -> p g n"),
             )
 
-        load_h2(0)
+        load_h2(0, pieces=PASSES)
+        load_w3_planes(0)
         nc.sync.dma_start(
             out=b3_rows[0 : E * PASSES, :], in_=b3.rearrange("e (h n) -> (e h) n", h=PASSES)
         )
-        nc.sync.dma_start(out=b4_row[0:1, :], in_=b4.rearrange("(o e) d -> o (e d)", o=1))
-        load_w3_planes(0)
         load_w3(0)
         load_h2(1)
+        load_w3(1)
+        nc.sync.dma_start(out=b4_row[0:1, :], in_=b4.rearrange("(o e) d -> o (e d)", o=1))
         load_w4_planes()
         load_w4(0)
-        load_w3(1)
         for a in range(1, E // 2):
             load_h2(2 * a)
             load_w3_planes(a)
@@ -128,39 +139,45 @@ def tile_environvectorfield_pb_e_kernel(
         h3_grouped_tiles = {}
         h3_mx = {}
 
-        def transpose_x(e, first_half_on_vector=False):
-            x_grouped = work.tile([P, PASSES * HALVES * P * PACK], BF16, align_bytes=64)
-            grouped_pairs = x_grouped[:].bitcast(F32).rearrange(
-                "p (g i b u) -> p g i b u", g=PASSES, i=HALVES, b=P
-            )
+        def transpose_x(e, copy_out):
+            x_grouped = work.tile([P, PASSES, HALVES * P * PACK], BF16, align_bytes=64)
             words_in_pass = K_PASS // 2
-            for i in range(HALVES):
-                x_pairs = h2_tiles[e][:, i, :].bitcast(F32)
-                xt = psum_tr.tile([P, PASSES, PAIR_WORDS, P], F32, tag="tr")
-                for g in range(PASSES):
+            for g in range(PASSES):
+                xt = psum_tr.tile([P, HALVES, PAIR_WORDS, P], F32, tag="tr")
+                for i in range(HALVES):
+                    x_pairs = h2_tiles[e][:, i, :].bitcast(F32)
                     for u in range(PAIR_WORDS):
                         nc.tensor.transpose(
-                            out=xt[:, g, u, :],
+                            out=xt[:, i, u, :],
                             in_=x_pairs[:, words_in_pass * g + u : words_in_pass * (g + 1) : PAIR_WORDS],
                             identity=ident[:],
                         )
-                dst = grouped_pairs[:, :, i, :, :]
-                src = xt[:].rearrange("p g u b -> p g b u")
-                if first_half_on_vector and i == 0:
-                    nc.vector.tensor_copy(out=dst, in_=src)
-                else:
-                    nc.scalar.copy(out=dst, in_=src)
+                copy_out(
+                    out=x_grouped[:, g, :].bitcast(F32).rearrange("p (i b u) -> p i b u", i=HALVES, b=P),
+                    in_=xt[:].rearrange("p i u b -> p i b u"),
+                )
             x_grouped_tiles[e] = x_grouped
 
-        def quantise(grouped, label):
+        def mx_tiles(label):
             words = work.tile([P, PASSES, HALVES, P], U32, align_bytes=64, tag=label + "_words")
             scales = work.tile([P, PASSES, HALVES, P], U8, align_bytes=64, tag=label + "_scales")
-            nc.vector.quantize_mx(
-                out=words[:].rearrange("p g i b -> p (g i b)").bitcast(FP8X4),
-                scales=scales[:].rearrange("p g i b -> p (g i b)"),
-                in_=grouped[:],
-            )
             return words, scales
+
+        def quantise(grouped, mx, passes):
+            words, scales = mx
+            nc.vector.quantize_mx(
+                out=words[:, passes, :, :].rearrange("p g i b -> p (g i b)").bitcast(FP8X4),
+                scales=scales[:, passes, :, :].rearrange("p g i b -> p (g i b)"),
+                in_=grouped[:, passes, :].rearrange("p g n -> p (g n)"),
+            )
+
+        def quantise_half(grouped, mx, h, i):
+            words, scales = mx
+            nc.vector.quantize_mx(
+                out=words[:, h, i, :].bitcast(FP8X4),
+                scales=scales[:, h, i, :],
+                in_=grouped[:, h, K_PASS * i : K_PASS * (i + 1)],
+            )
 
         def permute_w3_planes(a):
             nc.vector.tensor_copy(
@@ -172,25 +189,27 @@ def tile_environvectorfield_pb_e_kernel(
                 ),
             )
 
-        def permute_w3(e):
-            w3_perm = work.tile([P, PASSES, PASSES, PACK, P], U32, align_bytes=64)
-            for g in range(PASSES):
-                for h in range(PASSES):
-                    nc.vector.tensor_copy(
-                        out=w3_perm[:, g, h, :, :]
-                        .bitcast(I32)
-                        .rearrange("p t (c j) -> p c t j", j=4),
-                        in_=w3_tiles[e][:, g, K_PASS * h : K_PASS * (h + 1)]
-                        .bitcast(I32)
-                        .rearrange("p (c j t) -> p c t j", j=4, t=PACK),
-                    )
-            w3_perm_tiles[e] = w3_perm
+        def permute_w3(e, h):
+            if h == 0:
+                w3_perm = work.tile([P, PASSES, PASSES, PACK, P], U32, align_bytes=64)
+                w3_perm_tiles[e] = w3_perm
+            nc.vector.tensor_copy(
+                out=w3_perm_tiles[e][:, h, :, :, :]
+                .bitcast(I32)
+                .rearrange("p g t (c j) -> p g c t j", j=4),
+                in_=w3_tiles[e][:, :, K_PASS * h : K_PASS * (h + 1)]
+                .bitcast(I32)
+                .rearrange("p g (c j t) -> p g c t j", j=4, t=PACK),
+            )
 
         def stage1(e, h):
             words, scales = x_mx[e]
             if h == 0:
                 h3_planes = work.tile([P, PASSES, PACK, B], BF16)
                 h3_plane_tiles[e] = h3_planes
+                h3_grouped = work.tile([P, PASSES, B * PACK], BF16, align_bytes=64)
+                h3_grouped_tiles[e] = h3_grouped
+                h3_mx[e] = mx_tiles("h3")
             planes = h3_plane_tiles[e]
             for pair in range(PAIRS):
                 acc = psum_mx.tile([P, PACK // PAIRS, B], F32, tag="mx")
@@ -201,7 +220,7 @@ def tile_environvectorfield_pb_e_kernel(
                         a, c = divmod(PASSES * e + g, PLANES)
                         nc.tensor.matmul_mx(
                             out=acc[:, j, :],
-                            lhsT=w3_perm_tiles[e][:, g, h, t, :].bitcast(FP8X4),
+                            lhsT=w3_perm_tiles[e][:, h, g, t, :].bitcast(FP8X4),
                             lhsT_scale=w3_planes_perm[4 * c : P, a, cols],
                             rhs=words[:, g, :, :].rearrange("p i b -> p (i b)").bitcast(FP8X4),
                             rhs_scale=scales[:, g, :, :].rearrange("p i b -> p (i b)"),
@@ -218,30 +237,32 @@ def tile_environvectorfield_pb_e_kernel(
                         scale=1.0,
                     )
 
-        def regroup_h3(e, h):
-            if h == 0:
-                h3_grouped = work.tile([P, PASSES * B * PACK], BF16, align_bytes=64)
-                h3_grouped_tiles[e] = h3_grouped
-            grouped = h3_grouped_tiles[e][:].rearrange("p (h b t) -> p h b t", h=PASSES, t=PACK)
+        def regroup_h3(e, passes, rows):
+            words = slice(PACK * rows.start, PACK * rows.stop)
             nc.vector.tensor_copy(
-                out=grouped[:, h, :, :].rearrange("p (c j) t -> p c t j", j=4),
-                in_=h3_plane_tiles[e][:, h, :, :].rearrange("p t (c j) -> p c t j", j=4),
+                out=h3_grouped_tiles[e][:, passes, words].rearrange(
+                    "p h (c j t) -> p h c t j", j=4, t=PACK
+                ),
+                in_=h3_plane_tiles[e][:, passes, :, rows].rearrange("p h t (c j) -> p h c t j", j=4),
+            )
+
+        def stage2_pass(e, h, i, o):
+            words, scales = h3_mx[e]
+            nc.tensor.matmul_mx(
+                out=o,
+                lhsT=words[:, h, i, :].bitcast(FP8X4),
+                lhsT_scale=scales[:, h, i, :],
+                rhs=w4_sb[:, PASSES * e + h, :].bitcast(FP8X4),
+                rhs_scale=w4_planes[:, PASSES * e + h, :],
+                start=(h == 0),
+                stop=(h == PASSES - 1),
             )
 
         def stage2(e):
-            words, scales = h3_mx[e]
             o = psum_o.tile([P, HALVES, D], F32, tag="o")
             for i in range(HALVES):
                 for h in range(PASSES):
-                    nc.tensor.matmul_mx(
-                        out=o[:, i, :],
-                        lhsT=words[:, h, i, :].bitcast(FP8X4),
-                        lhsT_scale=scales[:, h, i, :],
-                        rhs=w4_sb[:, PASSES * e + h, :].bitcast(FP8X4),
-                        rhs_scale=w4_planes[:, PASSES * e + h, :],
-                        start=(h == 0),
-                        stop=(h == PASSES - 1),
-                    )
+                    stage2_pass(e, h, i, o[:, i, :])
             nc.vector.tensor_tensor(
                 out=out_sb[:, :, e, :],
                 in0=o[:],
@@ -250,47 +271,69 @@ def tile_environvectorfield_pb_e_kernel(
             )
             nc.sync.dma_start(out=out_by_env[:, :, e, :], in_=out_sb[:, :, e, :])
 
-        transpose_x(0, first_half_on_vector=True)
+        transpose_x(0, nc.scalar.copy)
 
         b3_sorted = const.tile([P, PACK, P], F32)
         nc.vector.tensor_copy(out=b3_sorted[:], in_=b3_rows[:].rearrange("r (p t) -> r t p", t=PACK))
-        x_mx[0] = quantise(x_grouped_tiles[0], "x")
-        permute_w3_planes(0)
-        b3_t = psum_tr.tile([P, PACK, P], F32, tag="tr")
+        b3_t = psum_o.tile([P, PACK, P], F32, tag="o")
         for t in range(PACK):
             nc.tensor.transpose(out=b3_t[:, t, :], in_=b3_sorted[:, t, :], identity=ident[:])
         b3_cols = const.tile([P, E * PASSES, PACK], F32)
-        nc.vector.tensor_copy(
-            out=b3_cols[:], in_=b3_t[:, :, 0 : E * PASSES].rearrange("p t r -> p r t")
-        )
-        b4_all = const.tile([P, E, D], F32)
-        for c in range(E * D // BANK):
-            b4_bank = psum_tr.tile([P, BANK], F32, tag="tr")
-            cols = slice(BANK * c, BANK * (c + 1))
-            nc.tensor.matmul(out=b4_bank[:], lhsT=ones[:], rhs=b4_row[:, cols], start=True, stop=True)
-            nc.scalar.copy(out=b4_all[:].rearrange("p e d -> p (e d)")[:, cols], in_=b4_bank[:])
-        permute_w3(0)
-        transpose_x(1)
+        nc.scalar.copy(out=b3_cols[:], in_=b3_t[:, :, 0 : E * PASSES].rearrange("p t r -> p r t"))
+        permute_w3_planes(0)
+        x_mx[0] = mx_tiles("x")
+        for n in range(PASSES):
+            quantise(x_grouped_tiles[0], x_mx[0], slice(n, n + 1))
+            permute_w3(0, n)
 
+        whole = slice(0, PASSES)
         for e in range(E):
             stage1(e, 0)
-            if e > 0:
-                for h in range(PASSES):
-                    regroup_h3(e - 1, h)
+            if e == 0:
+                transpose_x(1, nc.vector.tensor_copy)
+            stage1(e, 1)
+            if e == 0:
+                b4_all = const.tile([P, E, D], F32)
+                for c in range(E * D // BANK):
+                    b4_bank = psum_o.tile([P, BANK], F32, tag="o")
+                    cols = slice(BANK * c, BANK * (c + 1))
+                    nc.tensor.matmul(
+                        out=b4_bank[:], lhsT=ones[:], rhs=b4_row[:, cols], start=True, stop=True
+                    )
+                    nc.scalar.copy(
+                        out=b4_all[:].rearrange("p e d -> p (e d)")[:, cols], in_=b4_bank[:]
+                    )
             if e + 1 < E:
-                x_mx[e + 1] = quantise(x_grouped_tiles[e + 1], "x")
-            if e > 0:
-                h3_mx[e - 1] = quantise(h3_grouped_tiles[e - 1], "h3")
-            if e + 1 < E:
+                x_mx[e + 1] = mx_tiles("x")
+                quantise(x_grouped_tiles[e + 1], x_mx[e + 1], whole)
                 if (e + 1) % 2 == 0:
                     permute_w3_planes((e + 1) // 2)
-                permute_w3(e + 1)
-            stage1(e, 1)
-            if e > 0:
-                stage2(e - 1)
+                for h in range(PASSES):
+                    permute_w3(e + 1, h)
+            if e + 1 < E:
+                regroup_h3(e, whole, slice(0, B))
+                if e > 0:
+                    stage2(e - 1)
+                quantise(h3_grouped_tiles[e], h3_mx[e], whole)
             if e + 2 < E:
-                transpose_x(e + 2)
-        for h in range(PASSES):
-            regroup_h3(E - 1, h)
-        h3_mx[E - 1] = quantise(h3_grouped_tiles[E - 1], "h3")
-        stage2(E - 1)
+                transpose_x(e + 2, nc.scalar.copy)
+
+        e = E - 1
+        regroup_h3(e, slice(0, 1), slice(0, B))
+        stage2(e - 1)
+        quantise(h3_grouped_tiles[e], h3_mx[e], slice(0, 1))
+        for i in range(HALVES):
+            regroup_h3(e, slice(1, 2), slice(P * i, P * (i + 1)))
+        o_halves = []
+        for i in range(HALVES):
+            o_half = psum_tr.tile([P, D], F32, tag="tr")
+            o_halves.append(o_half)
+            stage2_pass(e, 0, i, o_half[:])
+        for i in range(HALVES):
+            quantise_half(h3_grouped_tiles[e], h3_mx[e], 1, i)
+            stage2_pass(e, 1, i, o_halves[i][:])
+        for i in range(HALVES):
+            nc.vector.tensor_tensor(
+                out=out_sb[:, i, e, :], in0=o_halves[i][:], in1=b4_all[:, e, :], op=ADD
+            )
+            nc.sync.dma_start(out=out_by_env[:, i, e, :], in_=out_sb[:, i, e, :])

@@ -84,12 +84,17 @@ def tile_environvectorfield_pb_e_kernel(
 
         def load_w3(e):
             w3_sb = w3_pool.tile([P, PASSES, H], U32, align_bytes=64)
-            for h in range(PASSES):
-                cols = slice(K_PASS * h, K_PASS * (h + 1))
-                nc.sync.dma_start(
-                    out=w3_sb[:, :, cols].bitcast(I32),
-                    in_=w3_words_dram[PASSES * e : PASSES * (e + 1), :, cols].rearrange("g p n -> p g n"),
-                )
+            for n in range(PASSES):
+                cols = slice(K_PASS * n, K_PASS * (n + 1))
+                if e == 0:
+                    nc.sync.dma_start(
+                        out=w3_sb[:, :, cols].bitcast(I32),
+                        in_=w3_words_dram[0:PASSES, :, cols].rearrange("g p n -> p g n"),
+                    )
+                else:
+                    nc.sync.dma_start(
+                        out=w3_sb[:, n, :].bitcast(I32), in_=w3_words_dram[PASSES * e + n]
+                    )
             w3_tiles[e] = w3_sb
 
         def load_w3_planes(a):
@@ -193,14 +198,15 @@ def tile_environvectorfield_pb_e_kernel(
             if h == 0:
                 w3_perm = work.tile([P, PASSES, PASSES, PACK, P], U32, align_bytes=64)
                 w3_perm_tiles[e] = w3_perm
-            nc.vector.tensor_copy(
-                out=w3_perm_tiles[e][:, h, :, :, :]
-                .bitcast(I32)
-                .rearrange("p g t (c j) -> p g c t j", j=4),
-                in_=w3_tiles[e][:, :, K_PASS * h : K_PASS * (h + 1)]
-                .bitcast(I32)
-                .rearrange("p g (c j t) -> p g c t j", j=4, t=PACK),
-            )
+            for g in range(PASSES):
+                nc.vector.tensor_copy(
+                    out=w3_perm_tiles[e][:, h, g, :, :]
+                    .bitcast(I32)
+                    .rearrange("p t (c j) -> p c t j", j=4),
+                    in_=w3_tiles[e][:, g, K_PASS * h : K_PASS * (h + 1)]
+                    .bitcast(I32)
+                    .rearrange("p (c j t) -> p c t j", j=4, t=PACK),
+                )
 
         def stage1(e, h):
             words, scales = x_mx[e]
@@ -237,13 +243,11 @@ def tile_environvectorfield_pb_e_kernel(
                         scale=1.0,
                     )
 
-        def regroup_h3(e, passes, rows):
+        def regroup_h3(e, h, rows):
             words = slice(PACK * rows.start, PACK * rows.stop)
             nc.vector.tensor_copy(
-                out=h3_grouped_tiles[e][:, passes, words].rearrange(
-                    "p h (c j t) -> p h c t j", j=4, t=PACK
-                ),
-                in_=h3_plane_tiles[e][:, passes, :, rows].rearrange("p h t (c j) -> p h c t j", j=4),
+                out=h3_grouped_tiles[e][:, h, words].rearrange("p (c j t) -> p c t j", j=4, t=PACK),
+                in_=h3_plane_tiles[e][:, h, :, rows].rearrange("p t (c j) -> p c t j", j=4),
             )
 
         def stage2_pass(e, h, i, o):
@@ -311,7 +315,8 @@ def tile_environvectorfield_pb_e_kernel(
                 for h in range(PASSES):
                     permute_w3(e + 1, h)
             if e + 1 < E:
-                regroup_h3(e, whole, slice(0, B))
+                for h in range(PASSES):
+                    regroup_h3(e, h, slice(0, B))
                 if e > 0:
                     stage2(e - 1)
                 quantise(h3_grouped_tiles[e], h3_mx[e], whole)
@@ -319,11 +324,11 @@ def tile_environvectorfield_pb_e_kernel(
                 transpose_x(e + 2, nc.scalar.copy)
 
         e = E - 1
-        regroup_h3(e, slice(0, 1), slice(0, B))
+        regroup_h3(e, 0, slice(0, B))
         stage2(e - 1)
         quantise(h3_grouped_tiles[e], h3_mx[e], slice(0, 1))
         for i in range(HALVES):
-            regroup_h3(e, slice(1, 2), slice(P * i, P * (i + 1)))
+            regroup_h3(e, 1, slice(P * i, P * (i + 1)))
         o_halves = []
         for i in range(HALVES):
             o_half = psum_tr.tile([P, D], F32, tag="tr")

@@ -33,7 +33,7 @@ def tile_environvectorfield_pb_e_kernel(
     nc = tc.nc
     with ExitStack() as ctx:
         const = ctx.enter_context(tc.tile_pool(name="const", bufs=1))
-        h2_pool = ctx.enter_context(tc.tile_pool(name="h2", bufs=E))
+        h2_pool = ctx.enter_context(tc.tile_pool(name="h2", bufs=1))
         w3_pool = ctx.enter_context(tc.tile_pool(name="w3", bufs=E))
         work = ctx.enter_context(tc.tile_pool(name="work", bufs=2))
         psum_mx = ctx.enter_context(tc.psum_pool(name="psum_mx", bufs=4))
@@ -63,38 +63,37 @@ def tile_environvectorfield_pb_e_kernel(
         nc.scalar.activation(out=warm_up[:], in_=warm_up[:], func=SILU, scale=1.0)
         nc.vector.memset(w3_planes[:, 0, :].bitcast(I32), 0)
         nc.vector.memset(b3_rows[:], 0.0)
+        nc.vector.memset(b4_row[:], 0.0)
         make_identity(nc, ident[:])
         nc.vector.memset(
             w3_planes[:, 1 : E * PASSES // PLANES, :].rearrange("p a n -> p (a n)").bitcast(I32), 0
         )
         nc.vector.memset(w4_planes[:].rearrange("p g d -> p (g d)").bitcast(I32), 0)
-        nc.vector.memset(b4_row[:], 0.0)
         nc.vector.memset(ones[:], 1.0)
 
         h2_tiles = {}
         w3_tiles = {}
 
-        def load_h2(e, pieces=1):
-            h2_sb = h2_pool.tile([P, HALVES, H], BF16)
+        def load_h2(first, envs, pieces=1):
+            h2_sb = h2_pool.tile([P, HALVES, envs, H], BF16, tag="h2_" + str(first))
             width = H // pieces
             for n in range(pieces):
                 cols = slice(width * n, width * (n + 1))
-                nc.sync.dma_start(out=h2_sb[:, :, cols], in_=h2_by_env[:, :, e, cols])
-            h2_tiles[e] = h2_sb
+                nc.sync.dma_start(
+                    out=h2_sb[:, :, :, cols], in_=h2_by_env[:, :, first : first + envs, cols]
+                )
+            for e in range(envs):
+                h2_tiles[first + e] = h2_sb[:, :, e, :]
 
-        def load_w3(e):
+        def load_w3(e, pieces=1):
             w3_sb = w3_pool.tile([P, PASSES, H], U32, align_bytes=64)
-            for n in range(PASSES):
-                cols = slice(K_PASS * n, K_PASS * (n + 1))
-                if e == 0:
-                    nc.sync.dma_start(
-                        out=w3_sb[:, :, cols].bitcast(I32),
-                        in_=w3_words_dram[0:PASSES, :, cols].rearrange("g p n -> p g n"),
-                    )
-                else:
-                    nc.sync.dma_start(
-                        out=w3_sb[:, n, :].bitcast(I32), in_=w3_words_dram[PASSES * e + n]
-                    )
+            width = H // pieces
+            for n in range(pieces):
+                cols = slice(width * n, width * (n + 1))
+                nc.sync.dma_start(
+                    out=w3_sb[:, :, cols].bitcast(I32),
+                    in_=w3_words_dram[PASSES * e : PASSES * (e + 1), :, cols].rearrange("g p n -> p g n"),
+                )
             w3_tiles[e] = w3_sb
 
         def load_w3_planes(a):
@@ -111,31 +110,41 @@ def tile_environvectorfield_pb_e_kernel(
                     in_=w4_scales_dram[:, 4 * quad : 4 * quad + 4, :].rearrange("g r d -> r g d"),
                 )
 
-        def load_w4(a):
-            passes = slice(PLANES * a, PLANES * (a + 1))
+        def load_w4(first, passes):
+            part = slice(first, first + passes)
             nc.sync.dma_start(
-                out=w4_sb[:, passes, :].bitcast(I32),
-                in_=w4_words_dram[passes].rearrange("g p n -> p g n"),
+                out=w4_sb[:, part, :].bitcast(I32), in_=w4_words_dram[part].rearrange("g p n -> p g n")
             )
 
-        load_h2(0, pieces=PASSES)
-        load_w3_planes(0)
-        nc.sync.dma_start(
+        nc.scalar.dma_start(
             out=b3_rows[0 : E * PASSES, :], in_=b3.rearrange("e (h n) -> (e h) n", h=PASSES)
         )
-        load_w3(0)
-        load_h2(1)
+        nc.scalar.dma_start(out=b4_row[0:1, :], in_=b4.rearrange("(o e) d -> o (e d)", o=1))
+        load_h2(0, 1, pieces=PASSES)
+        load_w3_planes(0)
+        load_w3(0, pieces=PASSES)
+        load_h2(1, 1)
         load_w3(1)
-        nc.sync.dma_start(out=b4_row[0:1, :], in_=b4.rearrange("(o e) d -> o (e d)", o=1))
+        load_h2(2, 1)
+        load_w3_planes(1)
+        load_w3(2)
         load_w4_planes()
-        load_w4(0)
-        for a in range(1, E // 2):
-            load_h2(2 * a)
-            load_w3_planes(a)
-            load_w4(a)
-            load_w3(2 * a)
-            load_h2(2 * a + 1)
-            load_w3(2 * a + 1)
+        load_w4(0 * PASSES, 2 * PASSES)
+        load_h2(3, 1)
+        load_w3(3)
+        load_w4(2 * PASSES, 2 * PASSES)
+        load_h2(4, 1)
+        load_w3_planes(2)
+        load_w3(4)
+        load_h2(5, 1)
+        load_w3(5)
+        load_w4(4 * PASSES, 2 * PASSES)
+        load_h2(6, 1)
+        load_w3_planes(3)
+        load_w3(6)
+        load_h2(7, 1)
+        load_w3(7)
+        load_w4(6 * PASSES, 2 * PASSES)
 
         x_grouped_tiles = {}
         x_mx = {}
@@ -198,15 +207,14 @@ def tile_environvectorfield_pb_e_kernel(
             if h == 0:
                 w3_perm = work.tile([P, PASSES, PASSES, PACK, P], U32, align_bytes=64)
                 w3_perm_tiles[e] = w3_perm
-            for g in range(PASSES):
-                nc.vector.tensor_copy(
-                    out=w3_perm_tiles[e][:, h, g, :, :]
-                    .bitcast(I32)
-                    .rearrange("p t (c j) -> p c t j", j=4),
-                    in_=w3_tiles[e][:, g, K_PASS * h : K_PASS * (h + 1)]
-                    .bitcast(I32)
-                    .rearrange("p (c j t) -> p c t j", j=4, t=PACK),
-                )
+            nc.vector.tensor_copy(
+                out=w3_perm_tiles[e][:, h, :, :, :]
+                .bitcast(I32)
+                .rearrange("p g t (c j) -> p g c t j", j=4),
+                in_=w3_tiles[e][:, :, K_PASS * h : K_PASS * (h + 1)]
+                .bitcast(I32)
+                .rearrange("p g (c j t) -> p g c t j", j=4, t=PACK),
+            )
 
         def stage1(e, h):
             words, scales = x_mx[e]
@@ -243,9 +251,9 @@ def tile_environvectorfield_pb_e_kernel(
                         scale=1.0,
                     )
 
-        def regroup_h3(e, h, rows):
+        def regroup_h3(e, h, rows, copy=nc.vector.tensor_copy):
             words = slice(PACK * rows.start, PACK * rows.stop)
-            nc.vector.tensor_copy(
+            copy(
                 out=h3_grouped_tiles[e][:, h, words].rearrange("p (c j t) -> p c t j", j=4, t=PACK),
                 in_=h3_plane_tiles[e][:, h, :, rows].rearrange("p t (c j) -> p c t j", j=4),
             )
@@ -296,6 +304,8 @@ def tile_environvectorfield_pb_e_kernel(
             if e == 0:
                 transpose_x(1, nc.vector.tensor_copy)
             stage1(e, 1)
+            if e + 1 < E:
+                regroup_h3(e, 0, slice(P, B), nc.scalar.copy)
             if e == 0:
                 b4_all = const.tile([P, E, D], F32)
                 for c in range(E * D // BANK):
@@ -315,8 +325,8 @@ def tile_environvectorfield_pb_e_kernel(
                 for h in range(PASSES):
                     permute_w3(e + 1, h)
             if e + 1 < E:
-                for h in range(PASSES):
-                    regroup_h3(e, h, slice(0, B))
+                regroup_h3(e, 0, slice(0, P))
+                regroup_h3(e, 1, slice(0, B))
                 if e > 0:
                     stage2(e - 1)
                 quantise(h3_grouped_tiles[e], h3_mx[e], whole)

@@ -116,13 +116,13 @@ def tile_environvectorfield_pb_e_kernel(
                 out=w4_sb[:, part, :].bitcast(I32), in_=w4_words_dram[part].rearrange("g p n -> p g n")
             )
 
-        nc.scalar.dma_start(
-            out=b3_rows[0 : E * PASSES, :], in_=b3.rearrange("e (h n) -> (e h) n", h=PASSES)
-        )
-        nc.scalar.dma_start(out=b4_row[0:1, :], in_=b4.rearrange("(o e) d -> o (e d)", o=1))
         load_h2(0, 1, pieces=PASSES)
         load_w3_planes(0)
+        nc.sync.dma_start(
+            out=b3_rows[0 : E * PASSES, :], in_=b3.rearrange("e (h n) -> (e h) n", h=PASSES)
+        )
         load_w3(0, pieces=PASSES)
+        nc.sync.dma_start(out=b4_row[0:1, :], in_=b4.rearrange("(o e) d -> o (e d)", o=1))
         load_h2(1, 1)
         load_w3(1)
         load_h2(2, 1)
@@ -302,11 +302,6 @@ def tile_environvectorfield_pb_e_kernel(
         for e in range(E):
             stage1(e, 0)
             if e == 0:
-                transpose_x(1, nc.vector.tensor_copy)
-            stage1(e, 1)
-            if e + 1 < E:
-                regroup_h3(e, 0, slice(P, B), nc.scalar.copy)
-            if e == 0:
                 b4_all = const.tile([P, E, D], F32)
                 for c in range(E * D // BANK):
                     b4_bank = psum_o.tile([P, BANK], F32, tag="o")
@@ -314,9 +309,13 @@ def tile_environvectorfield_pb_e_kernel(
                     nc.tensor.matmul(
                         out=b4_bank[:], lhsT=ones[:], rhs=b4_row[:, cols], start=True, stop=True
                     )
-                    nc.scalar.copy(
+                    nc.vector.tensor_copy(
                         out=b4_all[:].rearrange("p e d -> p (e d)")[:, cols], in_=b4_bank[:]
                     )
+                transpose_x(1, nc.vector.tensor_copy)
+            stage1(e, 1)
+            if e + 1 < E:
+                regroup_h3(e, 0, slice(192, B), nc.scalar.copy)
             if e + 1 < E:
                 x_mx[e + 1] = mx_tiles("x")
                 quantise(x_grouped_tiles[e + 1], x_mx[e + 1], whole)
@@ -325,7 +324,7 @@ def tile_environvectorfield_pb_e_kernel(
                 for h in range(PASSES):
                     permute_w3(e + 1, h)
             if e + 1 < E:
-                regroup_h3(e, 0, slice(0, P))
+                regroup_h3(e, 0, slice(0, 192))
                 regroup_h3(e, 1, slice(0, B))
                 if e > 0:
                     stage2(e - 1)
@@ -337,8 +336,8 @@ def tile_environvectorfield_pb_e_kernel(
         regroup_h3(e, 0, slice(0, B))
         stage2(e - 1)
         quantise(h3_grouped_tiles[e], h3_mx[e], slice(0, 1))
-        for i in range(HALVES):
-            regroup_h3(e, 1, slice(P * i, P * (i + 1)))
+        regroup_h3(e, 1, slice(0, P))
+        regroup_h3(e, 1, slice(P, B), nc.scalar.copy)
         o_halves = []
         for i in range(HALVES):
             o_half = psum_tr.tile([P, D], F32, tag="tr")

@@ -49,7 +49,7 @@ def tile_environvectorfield_pb_e_kernel(
         w4_scales_dram = W4_scales.bitcast(I32)
 
         w3_planes = const.tile([P, E * PASSES // PLANES, H], U8, align_bytes=64)
-        w3_planes_perm = const.tile([P, E * PASSES // PLANES, H], U8, align_bytes=64)
+        w3_planes_perm = const.tile([P, E * PASSES // PLANES, PACK, H // PACK], U8, align_bytes=64)
         w4_planes = const.tile([P, E * PASSES, D], U8, align_bytes=64)
         w4_sb = const.tile([P, E * PASSES, D], U32, align_bytes=64)
         b3_rows = const.tile([P, K_PASS], BF16)
@@ -143,7 +143,7 @@ def tile_environvectorfield_pb_e_kernel(
         load_w3_planes(3)
         load_w3(6)
         load_h2(7, 1)
-        load_w3(7)
+        load_w3(7, pieces=PASSES)
         load_w4(6 * PASSES, 2 * PASSES)
 
         x_grouped_tiles = {}
@@ -195,25 +195,21 @@ def tile_environvectorfield_pb_e_kernel(
 
         def permute_w3_planes(a):
             nc.vector.tensor_copy(
-                out=w3_planes_perm[:, a, :].rearrange(
-                    "p (h t c j) -> p h c t j", h=PASSES, t=PACK, j=16
-                ),
-                in_=w3_planes[:, a, :].rearrange(
-                    "p (h c j t) -> p h c t j", h=PASSES, t=PACK, j=16
-                ),
+                out=w3_planes_perm[:, a, :, :].rearrange("p t (c j) -> p c t j", j=16),
+                in_=w3_planes[:, a, :].rearrange("p (c j t) -> p c t j", j=16, t=PACK),
             )
 
-        def permute_w3(e, h):
-            if h == 0:
-                w3_perm = work.tile([P, PASSES, PASSES, PACK, P], U32, align_bytes=64)
+        def permute_w3(e, g, ms):
+            if e not in w3_perm_tiles:
+                w3_perm = work.tile([P, PASSES, PACK, H // PACK], U32, align_bytes=64)
                 w3_perm_tiles[e] = w3_perm
             nc.vector.tensor_copy(
-                out=w3_perm_tiles[e][:, h, :, :, :]
+                out=w3_perm_tiles[e][:, g, :, ms]
                 .bitcast(I32)
-                .rearrange("p g t (c j) -> p g c t j", j=4),
-                in_=w3_tiles[e][:, :, K_PASS * h : K_PASS * (h + 1)]
+                .rearrange("p t (c j) -> p c t j", j=4),
+                in_=w3_tiles[e][:, g, PACK * ms.start : PACK * ms.stop]
                 .bitcast(I32)
-                .rearrange("p g (c j t) -> p g c t j", j=4, t=PACK),
+                .rearrange("p (c j t) -> p c t j", j=4, t=PACK),
             )
 
         def stage1(e, h):
@@ -225,17 +221,17 @@ def tile_environvectorfield_pb_e_kernel(
                 h3_grouped_tiles[e] = h3_grouped
                 h3_mx[e] = mx_tiles("h3")
             planes = h3_plane_tiles[e]
+            ms = slice(P * h, P * (h + 1))
             for pair in range(PAIRS):
                 acc = psum_mx.tile([P, PACK // PAIRS, B], F32, tag="mx")
                 for j in range(PACK // PAIRS):
                     t = pair * (PACK // PAIRS) + j
-                    cols = slice(K_PASS * h + P * t, K_PASS * h + P * (t + 1))
                     for g in range(PASSES):
                         a, c = divmod(PASSES * e + g, PLANES)
                         nc.tensor.matmul_mx(
                             out=acc[:, j, :],
-                            lhsT=w3_perm_tiles[e][:, h, g, t, :].bitcast(FP8X4),
-                            lhsT_scale=w3_planes_perm[4 * c : P, a, cols],
+                            lhsT=w3_perm_tiles[e][:, g, t, ms].bitcast(FP8X4),
+                            lhsT_scale=w3_planes_perm[4 * c : P, a, t, ms],
                             rhs=words[:, g, :, :].rearrange("p i b -> p (i b)").bitcast(FP8X4),
                             rhs_scale=scales[:, g, :, :].rearrange("p i b -> p (i b)"),
                             start=(g == 0),
@@ -251,11 +247,18 @@ def tile_environvectorfield_pb_e_kernel(
                         scale=1.0,
                     )
 
-        def regroup_h3(e, h, rows, copy=nc.vector.tensor_copy):
+        def regroup_h3(e, h, rows):
             words = slice(PACK * rows.start, PACK * rows.stop)
-            copy(
+            nc.vector.tensor_copy(
                 out=h3_grouped_tiles[e][:, h, words].rearrange("p (c j t) -> p c t j", j=4, t=PACK),
                 in_=h3_plane_tiles[e][:, h, :, rows].rearrange("p t (c j) -> p c t j", j=4),
+            )
+
+        def regroup_h3_on_scalar(e, h, rows):
+            words = slice(PACK * rows.start, PACK * rows.stop)
+            nc.scalar.copy(
+                out=h3_grouped_tiles[e][:, h, words].rearrange("p (b t) -> p b t", t=PACK),
+                in_=h3_plane_tiles[e][:, h, :, rows].rearrange("p t b -> p b t"),
             )
 
         def stage2_pass(e, h, i, o):
@@ -296,7 +299,8 @@ def tile_environvectorfield_pb_e_kernel(
         x_mx[0] = mx_tiles("x")
         for n in range(PASSES):
             quantise(x_grouped_tiles[0], x_mx[0], slice(n, n + 1))
-            permute_w3(0, n)
+            for g in range(PASSES):
+                permute_w3(0, g, slice(P * n, P * (n + 1)))
 
         whole = slice(0, PASSES)
         for e in range(E):
@@ -315,14 +319,17 @@ def tile_environvectorfield_pb_e_kernel(
                 transpose_x(1, nc.vector.tensor_copy)
             stage1(e, 1)
             if e + 1 < E:
-                regroup_h3(e, 0, slice(192, B), nc.scalar.copy)
+                regroup_h3_on_scalar(e, 0, slice(192, B))
             if e + 1 < E:
                 x_mx[e + 1] = mx_tiles("x")
                 quantise(x_grouped_tiles[e + 1], x_mx[e + 1], whole)
                 if (e + 1) % 2 == 0:
                     permute_w3_planes((e + 1) // 2)
-                for h in range(PASSES):
-                    permute_w3(e + 1, h)
+                pieces = PASSES if e + 1 == E - 1 else 1
+                width = H // PACK // pieces
+                for n in range(pieces):
+                    for g in range(PASSES):
+                        permute_w3(e + 1, g, slice(width * n, width * (n + 1)))
             if e + 1 < E:
                 regroup_h3(e, 0, slice(0, 192))
                 regroup_h3(e, 1, slice(0, B))
@@ -337,7 +344,7 @@ def tile_environvectorfield_pb_e_kernel(
         stage2(e - 1)
         quantise(h3_grouped_tiles[e], h3_mx[e], slice(0, 1))
         regroup_h3(e, 1, slice(0, P))
-        regroup_h3(e, 1, slice(P, B), nc.scalar.copy)
+        regroup_h3_on_scalar(e, 1, slice(P, B))
         o_halves = []
         for i in range(HALVES):
             o_half = psum_tr.tile([P, D], F32, tag="tr")

@@ -36,6 +36,7 @@ def tile_environvectorfield_pb_e_kernel(
         h2_pool = ctx.enter_context(tc.tile_pool(name="h2", bufs=1))
         w3_pool = ctx.enter_context(tc.tile_pool(name="w3", bufs=E))
         work = ctx.enter_context(tc.tile_pool(name="work", bufs=2))
+        h3_pool = ctx.enter_context(tc.tile_pool(name="h3", bufs=E))
         psum_mx = ctx.enter_context(tc.psum_pool(name="psum_mx", bufs=4))
         psum_tr = ctx.enter_context(tc.psum_pool(name="psum_tr", bufs=2))
         psum_o = ctx.enter_context(tc.psum_pool(name="psum_o", bufs=2))
@@ -61,15 +62,15 @@ def tile_environvectorfield_pb_e_kernel(
         warm_up = const.tile([P, 1], F32)
         nc.vector.memset(warm_up[:], 0.0)
         nc.scalar.activation(out=warm_up[:], in_=warm_up[:], func=SILU, scale=1.0)
-        nc.vector.memset(w3_planes[:, 0, :].bitcast(I32), 0)
         nc.vector.memset(b3_rows[:], 0.0)
+        nc.vector.memset(w3_planes[:, 0, :].bitcast(I32), 0)
         nc.vector.memset(b4_row[:], 0.0)
+        nc.vector.memset(ones[:], 1.0)
         make_identity(nc, ident[:])
         nc.vector.memset(
             w3_planes[:, 1 : E * PASSES // PLANES, :].rearrange("p a n -> p (a n)").bitcast(I32), 0
         )
         nc.vector.memset(w4_planes[:].rearrange("p g d -> p (g d)").bitcast(I32), 0)
-        nc.vector.memset(ones[:], 1.0)
 
         h2_tiles = {}
         w3_tiles = {}
@@ -96,6 +97,14 @@ def tile_environvectorfield_pb_e_kernel(
                 )
             w3_tiles[e] = w3_sb
 
+        def load_w3_pass(e, g):
+            if g == 0:
+                w3_sb = w3_pool.tile([P, PASSES, H], U32, align_bytes=64)
+                w3_tiles[e] = w3_sb
+            nc.sync.dma_start(
+                out=w3_tiles[e][:, g, :].bitcast(I32), in_=w3_words_dram[PASSES * e + g]
+            )
+
         def load_w3_planes(a):
             for quad in range(QUADS):
                 nc.sync.dma_start(
@@ -117,34 +126,33 @@ def tile_environvectorfield_pb_e_kernel(
             )
 
         load_h2(0, 1, pieces=PASSES)
-        load_w3_planes(0)
         nc.sync.dma_start(
             out=b3_rows[0 : E * PASSES, :], in_=b3.rearrange("e (h n) -> (e h) n", h=PASSES)
         )
-        load_w3(0, pieces=PASSES)
+        load_w3_planes(0)
         nc.sync.dma_start(out=b4_row[0:1, :], in_=b4.rearrange("(o e) d -> o (e d)", o=1))
+        load_w3(0, pieces=PASSES)
         load_h2(1, 1)
-        load_w3(1)
+        load_w3_pass(1, 0)
+        load_w3_pass(1, 1)
         load_h2(2, 1)
         load_w3_planes(1)
         load_w3(2)
-        load_w4_planes()
-        load_w4(0 * PASSES, 2 * PASSES)
         load_h2(3, 1)
         load_w3(3)
-        load_w4(2 * PASSES, 2 * PASSES)
         load_h2(4, 1)
         load_w3_planes(2)
         load_w3(4)
         load_h2(5, 1)
         load_w3(5)
-        load_w4(4 * PASSES, 2 * PASSES)
         load_h2(6, 1)
         load_w3_planes(3)
         load_w3(6)
         load_h2(7, 1)
+        load_w4_planes()
+        load_w4(0 * PASSES, 4 * PASSES)
         load_w3(7, pieces=PASSES)
-        load_w4(6 * PASSES, 2 * PASSES)
+        load_w4(4 * PASSES, 4 * PASSES)
 
         x_grouped_tiles = {}
         x_mx = {}
@@ -173,8 +181,9 @@ def tile_environvectorfield_pb_e_kernel(
             x_grouped_tiles[e] = x_grouped
 
         def mx_tiles(label):
-            words = work.tile([P, PASSES, HALVES, P], U32, align_bytes=64, tag=label + "_words")
-            scales = work.tile([P, PASSES, HALVES, P], U8, align_bytes=64, tag=label + "_scales")
+            pool = h3_pool if label == "h3" else work
+            words = pool.tile([P, PASSES, HALVES, P], U32, align_bytes=64, tag=label + "_words")
+            scales = pool.tile([P, PASSES, HALVES, P], U8, align_bytes=64, tag=label + "_scales")
             return words, scales
 
         def quantise(grouped, mx, passes):
@@ -273,18 +282,23 @@ def tile_environvectorfield_pb_e_kernel(
                 stop=(h == PASSES - 1),
             )
 
-        def stage2(e):
-            o = psum_o.tile([P, HALVES, D], F32, tag="o")
-            for i in range(HALVES):
-                for h in range(PASSES):
-                    stage2_pass(e, h, i, o[:, i, :])
+        def stage2(first, envs):
+            o = psum_o.tile([P, HALVES, envs, D], F32, tag="o")
+            for e in range(envs):
+                for i in range(HALVES):
+                    for h in range(PASSES):
+                        stage2_pass(first + e, h, i, o[:, i, e, :])
+            part = slice(first, first + envs)
             nc.vector.tensor_tensor(
-                out=out_sb[:, :, e, :],
+                out=out_sb[:, :, part, :],
                 in0=o[:],
-                in1=b4_all[:, e, :].unsqueeze(1).to_broadcast([P, HALVES, D]),
+                in1=b4_all[:, part, :].unsqueeze(1).to_broadcast([P, HALVES, envs, D]),
                 op=ADD,
             )
-            nc.sync.dma_start(out=out_by_env[:, :, e, :], in_=out_sb[:, :, e, :])
+
+        def store(first, envs):
+            part = slice(first, first + envs)
+            nc.sync.dma_start(out=out_by_env[:, :, part, :], in_=out_sb[:, :, part, :])
 
         transpose_x(0, nc.scalar.copy)
 
@@ -295,33 +309,33 @@ def tile_environvectorfield_pb_e_kernel(
             nc.tensor.transpose(out=b3_t[:, t, :], in_=b3_sorted[:, t, :], identity=ident[:])
         b3_cols = const.tile([P, E * PASSES, PACK], F32)
         nc.scalar.copy(out=b3_cols[:], in_=b3_t[:, :, 0 : E * PASSES].rearrange("p t r -> p r t"))
-        permute_w3_planes(0)
         x_mx[0] = mx_tiles("x")
-        for n in range(PASSES):
-            quantise(x_grouped_tiles[0], x_mx[0], slice(n, n + 1))
-            for g in range(PASSES):
-                permute_w3(0, g, slice(P * n, P * (n + 1)))
+        quantise(x_grouped_tiles[0], x_mx[0], slice(0, 1))
+        permute_w3_planes(0)
+        permute_w3(0, 0, slice(0, P))
+        permute_w3(0, 1, slice(0, P))
+        quantise(x_grouped_tiles[0], x_mx[0], slice(1, 2))
+        permute_w3(0, 0, slice(P, 2 * P))
+        permute_w3(0, 1, slice(P, 2 * P))
+
+        b4_all = const.tile([P, E, D], F32)
+        for c in range(E * D // BANK):
+            b4_bank = psum_o.tile([P, BANK], F32, tag="o")
+            cols = slice(BANK * c, BANK * (c + 1))
+            nc.tensor.matmul(out=b4_bank[:], lhsT=ones[:], rhs=b4_row[:, cols], start=True, stop=True)
+            nc.scalar.copy(out=b4_all[:].rearrange("p e d -> p (e d)")[:, cols], in_=b4_bank[:])
 
         whole = slice(0, PASSES)
         for e in range(E):
             stage1(e, 0)
             if e == 0:
-                b4_all = const.tile([P, E, D], F32)
-                for c in range(E * D // BANK):
-                    b4_bank = psum_o.tile([P, BANK], F32, tag="o")
-                    cols = slice(BANK * c, BANK * (c + 1))
-                    nc.tensor.matmul(
-                        out=b4_bank[:], lhsT=ones[:], rhs=b4_row[:, cols], start=True, stop=True
-                    )
-                    nc.vector.tensor_copy(
-                        out=b4_all[:].rearrange("p e d -> p (e d)")[:, cols], in_=b4_bank[:]
-                    )
-                transpose_x(1, nc.vector.tensor_copy)
+                transpose_x(1, nc.scalar.copy)
             stage1(e, 1)
             if e + 1 < E:
                 regroup_h3_on_scalar(e, 0, slice(192, B))
-            if e + 1 < E:
                 x_mx[e + 1] = mx_tiles("x")
+                if e == 0:
+                    regroup_h3(e, 0, slice(0, 192))
                 quantise(x_grouped_tiles[e + 1], x_mx[e + 1], whole)
                 if (e + 1) % 2 == 0:
                     permute_w3_planes((e + 1) // 2)
@@ -330,21 +344,26 @@ def tile_environvectorfield_pb_e_kernel(
                 for n in range(pieces):
                     for g in range(PASSES):
                         permute_w3(e + 1, g, slice(width * n, width * (n + 1)))
-            if e + 1 < E:
-                regroup_h3(e, 0, slice(0, 192))
-                regroup_h3(e, 1, slice(0, B))
                 if e > 0:
-                    stage2(e - 1)
+                    regroup_h3(e, 0, slice(0, 192))
+                regroup_h3(e, 1, slice(0, B))
                 quantise(h3_grouped_tiles[e], h3_mx[e], whole)
             if e + 2 < E:
                 transpose_x(e + 2, nc.scalar.copy)
+            if e == E - 2:
+                stage2(0, 2)
+                stage2(2, 2)
+                store(0, 4)
 
         e = E - 1
         regroup_h3(e, 0, slice(0, B))
-        stage2(e - 1)
+        stage2(4, 2)
+        store(4, 2)
         quantise(h3_grouped_tiles[e], h3_mx[e], slice(0, 1))
         regroup_h3(e, 1, slice(0, P))
         regroup_h3_on_scalar(e, 1, slice(P, B))
+        stage2(6, 1)
+        store(6, 1)
         o_halves = []
         for i in range(HALVES):
             o_half = psum_tr.tile([P, D], F32, tag="tr")

@@ -204,8 +204,8 @@ def tile_environvectorfield_pb_e_kernel(
 
         def permute_w3_planes(a):
             nc.vector.tensor_copy(
-                out=w3_planes_perm[:, a, :, :].rearrange("p t (c j) -> p c t j", j=16),
-                in_=w3_planes[:, a, :].rearrange("p (c j t) -> p c t j", j=16, t=PACK),
+                out=w3_planes_perm[:, a, :, :].rearrange("p t (c j) -> p c t j", j=8),
+                in_=w3_planes[:, a, :].rearrange("p (c j t) -> p c t j", j=8, t=PACK),
             )
 
         def permute_w3(e, g, ms):
@@ -215,10 +215,10 @@ def tile_environvectorfield_pb_e_kernel(
             nc.vector.tensor_copy(
                 out=w3_perm_tiles[e][:, g, :, ms]
                 .bitcast(I32)
-                .rearrange("p t (c j) -> p c t j", j=4),
+                .rearrange("p t (c j) -> p c t j", j=2),
                 in_=w3_tiles[e][:, g, PACK * ms.start : PACK * ms.stop]
                 .bitcast(I32)
-                .rearrange("p (c j t) -> p c t j", j=4, t=PACK),
+                .rearrange("p (c j t) -> p c t j", j=2, t=PACK),
             )
 
         def stage1(e, h):

@@ -21,6 +21,7 @@ HALVES = B // P
 BANK = 512
 PAIRS = 2
 PLANES = 4
+LOADED = 8
 QUADS = 4
 PAIR_WORDS = 2
 
@@ -49,8 +50,9 @@ def tile_environvectorfield_pb_e_kernel(
         w3_scales_dram = W3_scales.bitcast(I32)
         w4_scales_dram = W4_scales.bitcast(I32)
 
-        w3_planes = const.tile([P, E * PASSES // PLANES, H], U8, align_bytes=64)
-        w3_planes_perm = const.tile([P, E * PASSES // PLANES, PACK, H // PACK], U8, align_bytes=64)
+        w3_planes = const.tile([P, E * PASSES // LOADED, H], U8, align_bytes=64)
+        w3_planes_perm = const.tile([P, E * PASSES // LOADED, PACK, H // PACK], U8, align_bytes=64)
+        w3_planes_high = const.tile([P, E * PASSES // LOADED, PACK, H // PACK], U8, align_bytes=64)
         w4_planes = const.tile([P, E * PASSES, D], U8, align_bytes=64)
         w4_sb = const.tile([P, E * PASSES, D], U32, align_bytes=64)
         b3_rows = const.tile([P, K_PASS], BF16)
@@ -63,13 +65,10 @@ def tile_environvectorfield_pb_e_kernel(
         nc.vector.memset(warm_up[:], 0.0)
         nc.scalar.activation(out=warm_up[:], in_=warm_up[:], func=SILU, scale=1.0)
         nc.vector.memset(b3_rows[:], 0.0)
-        nc.vector.memset(w3_planes[:, 0, :].bitcast(I32), 0)
         nc.vector.memset(b4_row[:], 0.0)
         nc.vector.memset(ones[:], 1.0)
         make_identity(nc, ident[:])
-        nc.vector.memset(
-            w3_planes[:, 1 : E * PASSES // PLANES, :].rearrange("p a n -> p (a n)").bitcast(I32), 0
-        )
+        nc.vector.memset(w3_planes_high[:].rearrange("p a t m -> p (a t m)").bitcast(I32), 0)
         nc.vector.memset(w4_planes[:].rearrange("p g d -> p (g d)").bitcast(I32), 0)
 
         h2_tiles = {}
@@ -108,8 +107,16 @@ def tile_environvectorfield_pb_e_kernel(
         def load_w3_planes(a):
             for quad in range(QUADS):
                 nc.sync.dma_start(
-                    out=w3_planes[32 * quad : 32 * quad + 16, a, :].bitcast(I32),
-                    in_=w3_scales_dram[PLANES * a : PLANES * (a + 1), 4 * quad : 4 * quad + 4, :],
+                    out=w3_planes[32 * quad : 32 * quad + 32, a, :].bitcast(I32),
+                    in_=w3_scales_dram[LOADED * a : LOADED * (a + 1), 4 * quad : 4 * quad + 4, :],
+                )
+
+        def lower_w3_planes(a):
+            for quad in range(QUADS):
+                low = 32 * quad
+                nc.sync.dma_start(
+                    out=w3_planes_high[low : low + 16, a, :, :].rearrange("p t m -> p (t m)").bitcast(I32),
+                    in_=w3_planes_perm[low + 16 : low + 32, a, :, :].rearrange("p t m -> p (t m)").bitcast(I32),
                 )
 
         def load_w4_planes():
@@ -135,24 +142,6 @@ def tile_environvectorfield_pb_e_kernel(
         load_h2(1, 1)
         load_w3_pass(1, 0)
         load_w3_pass(1, 1)
-        load_h2(2, 1)
-        load_w3_planes(1)
-        load_w3(2)
-        load_h2(3, 1)
-        load_w3(3)
-        load_h2(4, 1)
-        load_w3_planes(2)
-        load_w3(4)
-        load_h2(5, 1)
-        load_w3(5)
-        load_h2(6, 1)
-        load_w3_planes(3)
-        load_w3(6)
-        load_h2(7, 1)
-        load_w4_planes()
-        load_w4(0 * PASSES, 4 * PASSES)
-        load_w3(7, pieces=PASSES)
-        load_w4(4 * PASSES, 4 * PASSES)
 
         x_grouped_tiles = {}
         x_mx = {}
@@ -161,24 +150,24 @@ def tile_environvectorfield_pb_e_kernel(
         h3_grouped_tiles = {}
         h3_mx = {}
 
-        def transpose_x(e, copy_out):
-            x_grouped = work.tile([P, PASSES, HALVES * P * PACK], BF16, align_bytes=64)
+        def transpose_x(e, g, copy_out):
+            if g == 0:
+                x_grouped = work.tile([P, PASSES, HALVES * P * PACK], BF16, align_bytes=64)
+                x_grouped_tiles[e] = x_grouped
             words_in_pass = K_PASS // 2
-            for g in range(PASSES):
-                xt = psum_tr.tile([P, HALVES, PAIR_WORDS, P], F32, tag="tr")
-                for i in range(HALVES):
-                    x_pairs = h2_tiles[e][:, i, :].bitcast(F32)
-                    for u in range(PAIR_WORDS):
-                        nc.tensor.transpose(
-                            out=xt[:, i, u, :],
-                            in_=x_pairs[:, words_in_pass * g + u : words_in_pass * (g + 1) : PAIR_WORDS],
-                            identity=ident[:],
-                        )
-                copy_out(
-                    out=x_grouped[:, g, :].bitcast(F32).rearrange("p (i b u) -> p i b u", i=HALVES, b=P),
-                    in_=xt[:].rearrange("p i u b -> p i b u"),
-                )
-            x_grouped_tiles[e] = x_grouped
+            xt = psum_tr.tile([P, HALVES, PAIR_WORDS, P], F32, tag="tr")
+            for i in range(HALVES):
+                x_pairs = h2_tiles[e][:, i, :].bitcast(F32)
+                for u in range(PAIR_WORDS):
+                    nc.tensor.transpose(
+                        out=xt[:, i, u, :],
+                        in_=x_pairs[:, words_in_pass * g + u : words_in_pass * (g + 1) : PAIR_WORDS],
+                        identity=ident[:],
+                    )
+            copy_out(
+                out=x_grouped_tiles[e][:, g, :].bitcast(F32).rearrange("p (i b u) -> p i b u", i=HALVES, b=P),
+                in_=xt[:].rearrange("p i u b -> p i b u"),
+            )
 
         def mx_tiles(label):
             pool = h3_pool if label == "h3" else work
@@ -236,11 +225,13 @@ def tile_environvectorfield_pb_e_kernel(
                 for j in range(PACK // PAIRS):
                     t = pair * (PACK // PAIRS) + j
                     for g in range(PASSES):
-                        a, c = divmod(PASSES * e + g, PLANES)
+                        a, c = divmod(PASSES * e + g, LOADED)
+                        planes_of_pass = w3_planes_perm if c < PLANES else w3_planes_high
+                        c = c % PLANES
                         nc.tensor.matmul_mx(
                             out=acc[:, j, :],
                             lhsT=w3_perm_tiles[e][:, g, t, ms].bitcast(FP8X4),
-                            lhsT_scale=w3_planes_perm[4 * c : P, a, t, ms],
+                            lhsT_scale=planes_of_pass[4 * c : P, a, t, ms],
                             rhs=words[:, g, :, :].rearrange("p i b -> p (i b)").bitcast(FP8X4),
                             rhs_scale=scales[:, g, :, :].rearrange("p i b -> p (i b)"),
                             start=(g == 0),
@@ -300,7 +291,8 @@ def tile_environvectorfield_pb_e_kernel(
             part = slice(first, first + envs)
             nc.sync.dma_start(out=out_by_env[:, :, part, :], in_=out_sb[:, :, part, :])
 
-        transpose_x(0, nc.scalar.copy)
+        for g in range(PASSES):
+            transpose_x(0, g, nc.scalar.copy)
 
         b3_sorted = const.tile([P, PACK, P], F32)
         nc.vector.tensor_copy(out=b3_sorted[:], in_=b3_rows[:].rearrange("r (p t) -> r t p", t=PACK))
@@ -326,42 +318,79 @@ def tile_environvectorfield_pb_e_kernel(
             nc.scalar.copy(out=b4_all[:].rearrange("p e d -> p (e d)")[:, cols], in_=b4_bank[:])
 
         whole = slice(0, PASSES)
+        lower_w3_planes(0)
+        load_h2(2, 1)
+        load_w3_pass(2, 0)
+        load_w3_pass(2, 1)
+        load_h2(3, 1)
+        load_w3_planes(1)
+        load_w3(3)
+        load_h2(4, 1)
+        load_w3(4)
+        load_h2(5, 1)
+        load_w3(5)
+
+        SH = 192
+        def perm_step(e):
+            pieces = PASSES if e == E - 1 else 1
+            width = H // PACK // pieces
+            for n in range(pieces):
+                for g in range(PASSES):
+                    permute_w3(e, g, slice(width * n, width * (n + 1)))
+        def qx_step(e):
+            x_mx[e] = mx_tiles("x")
+            quantise(x_grouped_tiles[e], x_mx[e], whole)
         for e in range(E):
             stage1(e, 0)
             if e == 0:
-                transpose_x(1, nc.scalar.copy)
+                for g in range(PASSES):
+                    transpose_x(e + 1, g, nc.scalar.copy)
+            if e >= 9 and e + 2 < E:
+                transpose_x(e + 2, 0, nc.scalar.copy)
             stage1(e, 1)
             if e + 1 < E:
-                regroup_h3_on_scalar(e, 0, slice(192, B))
-                x_mx[e + 1] = mx_tiles("x")
+                regroup_h3_on_scalar(e, 0, slice(SH, B))
                 if e == 0:
-                    regroup_h3(e, 0, slice(0, 192))
-                quantise(x_grouped_tiles[e + 1], x_mx[e + 1], whole)
-                if (e + 1) % 2 == 0:
-                    permute_w3_planes((e + 1) // 2)
-                pieces = PASSES if e + 1 == E - 1 else 1
-                width = H // PACK // pieces
-                for n in range(pieces):
-                    for g in range(PASSES):
-                        permute_w3(e + 1, g, slice(width * n, width * (n + 1)))
+                    regroup_h3(e, 0, slice(0, SH))
+                if e + 1 == 2:
+                    permute_w3(e + 1, 0, slice(0, H // PACK))
+                    qx_step(e + 1)
+                    permute_w3(e + 1, 1, slice(0, H // PACK))
+                elif e + 1 >= 9:
+                    perm_step(e + 1)
+                    qx_step(e + 1)
+                else:
+                    qx_step(e + 1)
+                    perm_step(e + 1)
+                if e == 2:
+                    permute_w3_planes(1)
+                    lower_w3_planes(1)
+                    load_h2(6, 1)
+                    load_w3(6)
+                    load_h2(7, 1)
+                    load_w3(7, pieces=PASSES)
+                    load_w4_planes()
+                    load_w4(0 * PASSES, 4 * PASSES)
+                    load_w4(4 * PASSES, 4 * PASSES)
+
                 if e > 0:
-                    regroup_h3(e, 0, slice(0, 192))
+                    regroup_h3(e, 0, slice(0, SH))
                 regroup_h3(e, 1, slice(0, B))
                 quantise(h3_grouped_tiles[e], h3_mx[e], whole)
             if e + 2 < E:
-                transpose_x(e + 2, nc.scalar.copy)
-            if e == E - 2:
-                stage2(0, 2)
-                stage2(2, 2)
-                store(0, 4)
+                for g in range(1 if e >= 9 else 0, PASSES):
+                    transpose_x(e + 2, g, nc.scalar.copy)
 
         e = E - 1
         regroup_h3(e, 0, slice(0, B))
-        stage2(4, 2)
-        store(4, 2)
+        stage2(0, 2)
+        stage2(2, 2)
+        store(0, 4)
         quantise(h3_grouped_tiles[e], h3_mx[e], slice(0, 1))
         regroup_h3(e, 1, slice(0, P))
         regroup_h3_on_scalar(e, 1, slice(P, B))
+        stage2(4, 2)
+        store(4, 2)
         stage2(6, 1)
         store(6, 1)
         o_halves = []

@@ -371,7 +371,8 @@ def tile_environvectorfield_pb_e_kernel(
                     load_w3(7, pieces=PASSES)
                     load_w4_planes()
                     load_w4(0 * PASSES, 4 * PASSES)
-                    load_w4(4 * PASSES, 4 * PASSES)
+                    load_w4(4 * PASSES, 2 * PASSES)
+                    load_w4(6 * PASSES, 2 * PASSES)
 
                 if e > 0:
                     regroup_h3(e, 0, slice(0, SH))

@@ -27,7 +27,6 @@ PAIR_WORDS = 2
 
 FLOPS = 2 * B * E * H * (H + D)
 
-
 def tile_environvectorfield_pb_e_kernel(
     tc, h2, W3_words, W3_scales, b3, W4_words, W4_scales, b4, out
 ):
@@ -291,6 +290,13 @@ def tile_environvectorfield_pb_e_kernel(
             part = slice(first, first + envs)
             nc.sync.dma_start(out=out_by_env[:, :, part, :], in_=out_sb[:, :, part, :])
 
+        def keep_clock(n):
+            idle = psum_o.tile([P, BANK], F32, tag="o")
+            for c in range(n):
+                nc.tensor.matmul(
+                    out=idle[:], lhsT=ones[:], rhs=b4_row[:, 0:BANK], start=True, stop=True
+                )
+
         for g in range(PASSES):
             transpose_x(0, g, nc.scalar.copy)
 
@@ -340,16 +346,29 @@ def tile_environvectorfield_pb_e_kernel(
         def qx_step(e):
             x_mx[e] = mx_tiles("x")
             quantise(x_grouped_tiles[e], x_mx[e], whole)
+        def tx(e):
+            for g in range(PASSES):
+                transpose_x(e, g, nc.scalar.copy)
+        T2 = "pre"
         for e in range(E):
+            if e == 1 and T2 == "pre":
+                keep_clock(3)
+                tx(2)
             stage1(e, 0)
             if e == 0:
-                for g in range(PASSES):
-                    transpose_x(e + 1, g, nc.scalar.copy)
-            if e >= 9 and e + 2 < E:
-                transpose_x(e + 2, 0, nc.scalar.copy)
+                tx(1)
+            if e == 1 and T2 == "mid":
+                tx(2)
+            if e == 1 and T2 == "half":
+                transpose_x(2, 0, nc.scalar.copy)
             stage1(e, 1)
+            if e == 1 and T2 == "half":
+                transpose_x(2, 1, nc.scalar.copy)
+            if e == 1 and T2 == "post":
+                tx(2)
             if e + 1 < E:
-                regroup_h3_on_scalar(e, 0, slice(SH, B))
+                if SH < B:
+                    regroup_h3_on_scalar(e, 0, slice(SH, B))
                 if e == 0:
                     regroup_h3(e, 0, slice(0, SH))
                 if e + 1 == 2:
@@ -377,10 +396,11 @@ def tile_environvectorfield_pb_e_kernel(
                 if e > 0:
                     regroup_h3(e, 0, slice(0, SH))
                 regroup_h3(e, 1, slice(0, B))
-                quantise(h3_grouped_tiles[e], h3_mx[e], whole)
-            if e + 2 < E:
-                for g in range(1 if e >= 9 else 0, PASSES):
-                    transpose_x(e + 2, g, nc.scalar.copy)
+                for h in range(PASSES):
+                    quantise(h3_grouped_tiles[e], h3_mx[e], slice(h, h + 1))
+            if 0 < e and e + 2 < E:
+                tx(e + 2)
+
 
         e = E - 1
         regroup_h3(e, 0, slice(0, B))

@@ -336,7 +336,7 @@ def tile_environvectorfield_pb_e_kernel(
         load_h2(5, 1)
         load_w3(5)
 
-        SH = 192
+        SH = 224
         def perm_step(e):
             pieces = PASSES if e == E - 1 else 1
             width = H // PACK // pieces
@@ -405,10 +405,11 @@ def tile_environvectorfield_pb_e_kernel(
         e = E - 1
         regroup_h3(e, 0, slice(0, B))
         stage2(0, 2)
+        store(0, 2)
         stage2(2, 2)
-        store(0, 4)
+        store(2, 2)
         quantise(h3_grouped_tiles[e], h3_mx[e], slice(0, 1))
-        regroup_h3(e, 1, slice(0, P))
+        regroup_h3_on_scalar(e, 1, slice(0, P))
         regroup_h3_on_scalar(e, 1, slice(P, B))
         stage2(4, 2)
         store(4, 2)

@@ -73,6 +73,12 @@ def tile_environvectorfield_pb_e_kernel(
         h2_tiles = {}
         w3_tiles = {}
 
+        def load_h2_half(i):
+            if i == 0:
+                h2_first = h2_pool.tile([P, HALVES, H], BF16, tag="h2_0")
+                h2_tiles[0] = h2_first
+            nc.sync.dma_start(out=h2_tiles[0][:, i, :], in_=h2_by_env[:, i, 0, :])
+
         def load_h2(first, envs, pieces=1):
             h2_sb = h2_pool.tile([P, HALVES, envs, H], BF16, tag="h2_" + str(first))
             width = H // pieces
@@ -131,7 +137,8 @@ def tile_environvectorfield_pb_e_kernel(
                 out=w4_sb[:, part, :].bitcast(I32), in_=w4_words_dram[part].rearrange("g p n -> p g n")
             )
 
-        load_h2(0, 1, pieces=PASSES)
+        load_h2_half(0)
+        load_h2_half(1)
         nc.sync.dma_start(
             out=b3_rows[0 : E * PASSES, :], in_=b3.rearrange("e (h n) -> (e h) n", h=PASSES)
         )
@@ -140,6 +147,7 @@ def tile_environvectorfield_pb_e_kernel(
         load_w3(0, pieces=PASSES)
         load_h2(1, 1)
         load_w3_pass(1, 0)
+        load_h2(2, 1)
         load_w3_pass(1, 1)
 
         x_grouped_tiles = {}
@@ -272,12 +280,15 @@ def tile_environvectorfield_pb_e_kernel(
                 stop=(h == PASSES - 1),
             )
 
-        def stage2(first, envs):
-            o = psum_o.tile([P, HALVES, envs, D], F32, tag="o")
+        def stage2(first, envs, pool, tag):
+            o = pool.tile([P, HALVES, envs, D], F32, tag=tag)
             for e in range(envs):
                 for i in range(HALVES):
                     for h in range(PASSES):
                         stage2_pass(first + e, h, i, o[:, i, e, :])
+            return o
+
+        def add_b4(o, first, envs):
             part = slice(first, first + envs)
             nc.vector.tensor_tensor(
                 out=out_sb[:, :, part, :],
@@ -297,8 +308,22 @@ def tile_environvectorfield_pb_e_kernel(
                     out=idle[:], lhsT=ones[:], rhs=b4_row[:, 0:BANK], start=True, stop=True
                 )
 
-        for g in range(PASSES):
-            transpose_x(0, g, nc.scalar.copy)
+        x_grouped = work.tile([P, PASSES, HALVES * P * PACK], BF16, align_bytes=64, tag="x_grouped")
+        x_grouped_tiles[0] = x_grouped
+        for i in range(HALVES):
+            xt = psum_tr.tile([P, PASSES, PAIR_WORDS, P], F32, tag="tr")
+            x_pairs = h2_tiles[0][:, i, :].bitcast(F32)
+            for g in range(PASSES):
+                for u in range(PAIR_WORDS):
+                    nc.tensor.transpose(
+                        out=xt[:, g, u, :],
+                        in_=x_pairs[:, K_PASS // 2 * g + u : K_PASS // 2 * (g + 1) : PAIR_WORDS],
+                        identity=ident[:],
+                    )
+            nc.scalar.copy(
+                out=x_grouped[:, :, K_PASS * i : K_PASS * (i + 1)].bitcast(F32).rearrange("p g (b u) -> p g b u", b=P),
+                in_=xt[:].rearrange("p g u b -> p g b u"),
+            )
 
         b3_sorted = const.tile([P, PACK, P], F32)
         nc.vector.tensor_copy(out=b3_sorted[:], in_=b3_rows[:].rearrange("r (p t) -> r t p", t=PACK))
@@ -308,11 +333,13 @@ def tile_environvectorfield_pb_e_kernel(
         b3_cols = const.tile([P, E * PASSES, PACK], F32)
         nc.scalar.copy(out=b3_cols[:], in_=b3_t[:, :, 0 : E * PASSES].rearrange("p t r -> p r t"))
         x_mx[0] = mx_tiles("x")
-        quantise(x_grouped_tiles[0], x_mx[0], slice(0, 1))
+        for g in range(PASSES):
+            quantise_half(x_grouped, x_mx[0], g, 0)
         permute_w3_planes(0)
         permute_w3(0, 0, slice(0, P))
         permute_w3(0, 1, slice(0, P))
-        quantise(x_grouped_tiles[0], x_mx[0], slice(1, 2))
+        for g in range(PASSES):
+            quantise_half(x_grouped, x_mx[0], g, 1)
         permute_w3(0, 0, slice(P, 2 * P))
         permute_w3(0, 1, slice(P, 2 * P))
 
@@ -325,18 +352,24 @@ def tile_environvectorfield_pb_e_kernel(
 
         whole = slice(0, PASSES)
         lower_w3_planes(0)
-        load_h2(2, 1)
         load_w3_pass(2, 0)
-        load_w3_pass(2, 1)
         load_h2(3, 1)
-        load_w3_planes(1)
-        load_w3(3)
+        load_w3_pass(2, 1)
+        load_w3_pass(3, 0)
         load_h2(4, 1)
-        load_w3(4)
+        load_w3_pass(3, 1)
+        load_w3_planes(1)
+        load_w3_pass(4, 0)
         load_h2(5, 1)
-        load_w3(5)
+        load_w3_pass(4, 1)
+        load_w3_pass(5, 0)
+        load_h2(6, 1)
+        load_w3_pass(5, 1)
+        load_h2(7, 1)
+        load_w3_pass(6, 0)
+        load_w3_pass(6, 1)
 
-        SH = 224
+        SH = 208
         def perm_step(e):
             pieces = PASSES if e == E - 1 else 1
             width = H // PACK // pieces
@@ -352,7 +385,6 @@ def tile_environvectorfield_pb_e_kernel(
         T2 = "pre"
         for e in range(E):
             if e == 1 and T2 == "pre":
-                keep_clock(3)
                 tx(2)
             stage1(e, 0)
             if e == 0:
@@ -371,7 +403,17 @@ def tile_environvectorfield_pb_e_kernel(
                     regroup_h3_on_scalar(e, 0, slice(SH, B))
                 if e == 0:
                     regroup_h3(e, 0, slice(0, SH))
-                if e + 1 == 2:
+                if e == 3:
+                    permute_w3_planes(1)
+                    lower_w3_planes(1)
+                    load_w3(7, pieces=PASSES)
+                    load_w4_planes()
+                    load_w4(0 * PASSES, 2 * PASSES)
+                    load_w4(2 * PASSES, 2 * PASSES)
+                    load_w4(4 * PASSES, 2 * PASSES)
+                    load_w4(6 * PASSES, 2 * PASSES)
+
+                if e + 1 in (1, 2, 3, 4, 5, 6):
                     permute_w3(e + 1, 0, slice(0, H // PACK))
                     qx_step(e + 1)
                     permute_w3(e + 1, 1, slice(0, H // PACK))
@@ -381,18 +423,6 @@ def tile_environvectorfield_pb_e_kernel(
                 else:
                     qx_step(e + 1)
                     perm_step(e + 1)
-                if e == 2:
-                    permute_w3_planes(1)
-                    lower_w3_planes(1)
-                    load_h2(6, 1)
-                    load_w3(6)
-                    load_h2(7, 1)
-                    load_w3(7, pieces=PASSES)
-                    load_w4_planes()
-                    load_w4(0 * PASSES, 4 * PASSES)
-                    load_w4(4 * PASSES, 2 * PASSES)
-                    load_w4(6 * PASSES, 2 * PASSES)
-
                 if e > 0:
                     regroup_h3(e, 0, slice(0, SH))
                 regroup_h3(e, 1, slice(0, B))
@@ -401,20 +431,21 @@ def tile_environvectorfield_pb_e_kernel(
             if 0 < e and e + 2 < E:
                 tx(e + 2)
 
-
         e = E - 1
+        o01 = stage2(0, 2, psum_o, "o")
+        o23 = stage2(2, 2, psum_o, "o")
+        o45 = stage2(4, 2, psum_mx, "mx")
+        o6 = stage2(6, 1, psum_mx, "mx")
         regroup_h3(e, 0, slice(0, B))
-        stage2(0, 2)
+        add_b4(o01, 0, 2)
         store(0, 2)
-        stage2(2, 2)
+        add_b4(o23, 2, 2)
         store(2, 2)
         quantise(h3_grouped_tiles[e], h3_mx[e], slice(0, 1))
-        regroup_h3_on_scalar(e, 1, slice(0, P))
-        regroup_h3_on_scalar(e, 1, slice(P, B))
-        stage2(4, 2)
+        add_b4(o45, 4, 2)
         store(4, 2)
-        stage2(6, 1)
-        store(6, 1)
+        for i in range(HALVES):
+            regroup_h3_on_scalar(e, 1, slice(P * i, P * (i + 1)))
         o_halves = []
         for i in range(HALVES):
             o_half = psum_tr.tile([P, D], F32, tag="tr")
@@ -423,6 +454,8 @@ def tile_environvectorfield_pb_e_kernel(
         for i in range(HALVES):
             quantise_half(h3_grouped_tiles[e], h3_mx[e], 1, i)
             stage2_pass(e, 1, i, o_halves[i][:])
+        add_b4(o6, 6, 1)
+        store(6, 1)
         for i in range(HALVES):
             nc.vector.tensor_tensor(
                 out=out_sb[:, i, e, :], in0=o_halves[i][:], in1=b4_all[:, e, :], op=ADD

from contextlib import ExitStack

import concourse.mybir as mybir
from concourse.masks import make_identity

F32 = mybir.dt.float32
BF16 = mybir.dt.bfloat16
U8 = mybir.dt.uint8
U32 = mybir.dt.uint32
I32 = mybir.dt.int32
FP8X4 = mybir.dt.float8_e4m3fn_x4
SILU = mybir.ActivationFunctionType.Silu
ADD = mybir.AluOpType.add

B, E, H, D = 256, 8, 1024, 128
P = 128
PACK = 4
K_PASS = P * PACK
PASSES = H // K_PASS
HALVES = B // P
BANK = 512
PAIRS = 2
PLANES = 4
LOADED = 8
QUADS = 4
PAIR_WORDS = 2

FLOPS = 2 * B * E * H * (H + D)

def tile_environvectorfield_pb_e_kernel(
    tc, h2, W3_words, W3_scales, b3, W4_words, W4_scales, b4, out
):
    nc = tc.nc
    with ExitStack() as ctx:
        const = ctx.enter_context(tc.tile_pool(name="const", bufs=1))
        h2_pool = ctx.enter_context(tc.tile_pool(name="h2", bufs=1))
        w3_pool = ctx.enter_context(tc.tile_pool(name="w3", bufs=E))
        work = ctx.enter_context(tc.tile_pool(name="work", bufs=2))
        h3_pool = ctx.enter_context(tc.tile_pool(name="h3", bufs=E))
        psum_mx = ctx.enter_context(tc.psum_pool(name="psum_mx", bufs=4))
        psum_tr = ctx.enter_context(tc.psum_pool(name="psum_tr", bufs=2))
        psum_o = ctx.enter_context(tc.psum_pool(name="psum_o", bufs=2))
        ctx.enter_context(tc.manual_schedule())

        h2_by_env = h2.rearrange("(p i) e k -> p i e k", i=HALVES)
        out_by_env = out.rearrange("(p i e) d -> p i e d", i=HALVES, e=E)
        w3_words_dram = W3_words.rearrange("g p n t -> g p (n t)").bitcast(I32)
        w4_words_dram = W4_words.rearrange("g p n t -> g p (n t)").bitcast(I32)
        w3_scales_dram = W3_scales.bitcast(I32)
        w4_scales_dram = W4_scales.bitcast(I32)

        w3_planes = const.tile([P, E * PASSES // LOADED, H], U8, align_bytes=64)
        w3_planes_perm = const.tile([P, E * PASSES // LOADED, PACK, H // PACK], U8, align_bytes=64)
        w3_planes_high = const.tile([P, E * PASSES // LOADED, PACK, H // PACK], U8, align_bytes=64)
        w4_planes = const.tile([P, E * PASSES, D], U8, align_bytes=64)
        w4_sb = const.tile([P, E * PASSES, D], U32, align_bytes=64)
        b3_rows = const.tile([P, K_PASS], BF16)
        b4_row = const.tile([P, E * D], BF16)
        ones = const.tile([P, P], BF16)
        ident = const.tile([P, P], F32)
        out_sb = const.tile([P, HALVES, E, D], F32)

        warm_up = const.tile([P, 1], F32)
        nc.vector.memset(warm_up[:], 0.0)
        nc.scalar.activation(out=warm_up[:], in_=warm_up[:], func=SILU, scale=1.0)
        nc.vector.memset(b3_rows[:], 0.0)
        nc.vector.memset(b4_row[:], 0.0)
        nc.vector.memset(ones[:], 1.0)
        make_identity(nc, ident[:])
        nc.vector.memset(w3_planes_high[:].rearrange("p a t m -> p (a t m)").bitcast(I32), 0)
        nc.vector.memset(w4_planes[:].rearrange("p g d -> p (g d)").bitcast(I32), 0)

        h2_tiles = {}
        w3_tiles = {}

        def load_h2_half(i):
            if i == 0:
                h2_first = h2_pool.tile([P, HALVES, H], BF16, tag="h2_0")
                h2_tiles[0] = h2_first
            nc.sync.dma_start(out=h2_tiles[0][:, i, :], in_=h2_by_env[:, i, 0, :])

        def load_h2(first, envs, pieces=1):
            h2_sb = h2_pool.tile([P, HALVES, envs, H], BF16, tag="h2_" + str(first))
            width = H // pieces
            for n in range(pieces):
                cols = slice(width * n, width * (n + 1))
                nc.sync.dma_start(
                    out=h2_sb[:, :, :, cols], in_=h2_by_env[:, :, first : first + envs, cols]
                )
            for e in range(envs):
                h2_tiles[first + e] = h2_sb[:, :, e, :]

        def load_w3(e, pieces=1):
            w3_sb = w3_pool.tile([P, PASSES, H], U32, align_bytes=64)
            width = H // pieces
            for n in range(pieces):
                cols = slice(width * n, width * (n + 1))
                nc.sync.dma_start(
                    out=w3_sb[:, :, cols].bitcast(I32),
                    in_=w3_words_dram[PASSES * e : PASSES * (e + 1), :, cols].rearrange("g p n -> p g n"),
                )
            w3_tiles[e] = w3_sb

        def load_w3_pass(e, g):
            if g == 0:
                w3_sb = w3_pool.tile([P, PASSES, H], U32, align_bytes=64)
                w3_tiles[e] = w3_sb
            nc.sync.dma_start(
                out=w3_tiles[e][:, g, :].bitcast(I32), in_=w3_words_dram[PASSES * e + g]
            )

        def load_w3_planes(a):
            for quad in range(QUADS):
                nc.sync.dma_start(
                    out=w3_planes[32 * quad : 32 * quad + 32, a, :].bitcast(I32),
                    in_=w3_scales_dram[LOADED * a : LOADED * (a + 1), 4 * quad : 4 * quad + 4, :],
                )

        def lower_w3_planes(a):
            for quad in range(QUADS):
                low = 32 * quad
                nc.sync.dma_start(
                    out=w3_planes_high[low : low + 16, a, :, :].rearrange("p t m -> p (t m)").bitcast(I32),
                    in_=w3_planes_perm[low + 16 : low + 32, a, :, :].rearrange("p t m -> p (t m)").bitcast(I32),
                )

        def load_w4_planes():
            for quad in range(QUADS):
                nc.sync.dma_start(
                    out=w4_planes[32 * quad : 32 * quad + 4, :, :].bitcast(I32),
                    in_=w4_scales_dram[:, 4 * quad : 4 * quad + 4, :].rearrange("g r d -> r g d"),
                )

        def load_w4(first, passes):
            part = slice(first, first + passes)
            nc.sync.dma_start(
                out=w4_sb[:, part, :].bitcast(I32), in_=w4_words_dram[part].rearrange("g p n -> p g n")
            )

        load_h2_half(0)
        load_h2_half(1)
        nc.sync.dma_start(
            out=b3_rows[0 : E * PASSES, :], in_=b3.rearrange("e (h n) -> (e h) n", h=PASSES)
        )
        load_w3_planes(0)
        nc.sync.dma_start(out=b4_row[0:1, :], in_=b4.rearrange("(o e) d -> o (e d)", o=1))
        load_w3(0, pieces=PASSES)
        load_h2(1, 1)
        load_w3_pass(1, 0)
        load_h2(2, 1)
        load_w3_pass(1, 1)

        x_grouped_tiles = {}
        x_mx = {}
        w3_perm_tiles = {}
        h3_plane_tiles = {}
        h3_grouped_tiles = {}
        h3_mx = {}

        def transpose_x(e, g, copy_out):
            if g == 0:
                x_grouped = work.tile([P, PASSES, HALVES * P * PACK], BF16, align_bytes=64)
                x_grouped_tiles[e] = x_grouped
            words_in_pass = K_PASS // 2
            xt = psum_tr.tile([P, HALVES, PAIR_WORDS, P], F32, tag="tr")
            for i in range(HALVES):
                x_pairs = h2_tiles[e][:, i, :].bitcast(F32)
                for u in range(PAIR_WORDS):
                    nc.tensor.transpose(
                        out=xt[:, i, u, :],
                        in_=x_pairs[:, words_in_pass * g + u : words_in_pass * (g + 1) : PAIR_WORDS],
                        identity=ident[:],
                    )
            copy_out(
                out=x_grouped_tiles[e][:, g, :].bitcast(F32).rearrange("p (i b u) -> p i b u", i=HALVES, b=P),
                in_=xt[:].rearrange("p i u b -> p i b u"),
            )

        def mx_tiles(label):
            pool = h3_pool if label == "h3" else work
            words = pool.tile([P, PASSES, HALVES, P], U32, align_bytes=64, tag=label + "_words")
            scales = pool.tile([P, PASSES, HALVES, P], U8, align_bytes=64, tag=label + "_scales")
            return words, scales

        def quantise(grouped, mx, passes):
            words, scales = mx
            nc.vector.quantize_mx(
                out=words[:, passes, :, :].rearrange("p g i b -> p (g i b)").bitcast(FP8X4),
                scales=scales[:, passes, :, :].rearrange("p g i b -> p (g i b)"),
                in_=grouped[:, passes, :].rearrange("p g n -> p (g n)"),
            )

        def quantise_half(grouped, mx, h, i):
            words, scales = mx
            nc.vector.quantize_mx(
                out=words[:, h, i, :].bitcast(FP8X4),
                scales=scales[:, h, i, :],
                in_=grouped[:, h, K_PASS * i : K_PASS * (i + 1)],
            )

        def permute_w3_planes(a):
            nc.vector.tensor_copy(
                out=w3_planes_perm[:, a, :, :].rearrange("p t (c j) -> p c t j", j=8),
                in_=w3_planes[:, a, :].rearrange("p (c j t) -> p c t j", j=8, t=PACK),
            )

        def permute_w3(e, g, ms):
            if e not in w3_perm_tiles:
                w3_perm = work.tile([P, PASSES, PACK, H // PACK], U32, align_bytes=64)
                w3_perm_tiles[e] = w3_perm
            nc.vector.tensor_copy(
                out=w3_perm_tiles[e][:, g, :, ms]
                .bitcast(I32)
                .rearrange("p t (c j) -> p c t j", j=2),
                in_=w3_tiles[e][:, g, PACK * ms.start : PACK * ms.stop]
                .bitcast(I32)
                .rearrange("p (c j t) -> p c t j", j=2, t=PACK),
            )

        def stage1(e, h):
            words, scales = x_mx[e]
            if h == 0:
                h3_planes = work.tile([P, PASSES, PACK, B], BF16)
                h3_plane_tiles[e] = h3_planes
                h3_grouped = work.tile([P, PASSES, B * PACK], BF16, align_bytes=64)
                h3_grouped_tiles[e] = h3_grouped
                h3_mx[e] = mx_tiles("h3")
            planes = h3_plane_tiles[e]
            ms = slice(P * h, P * (h + 1))
            for pair in range(PAIRS):
                acc = psum_mx.tile([P, PACK // PAIRS, B], F32, tag="mx")
                for j in range(PACK // PAIRS):
                    t = pair * (PACK // PAIRS) + j
                    for g in range(PASSES):
                        a, c = divmod(PASSES * e + g, LOADED)
                        planes_of_pass = w3_planes_perm if c < PLANES else w3_planes_high
                        c = c % PLANES
                        nc.tensor.matmul_mx(
                            out=acc[:, j, :],
                            lhsT=w3_perm_tiles[e][:, g, t, ms].bitcast(FP8X4),
                            lhsT_scale=planes_of_pass[4 * c : P, a, t, ms],
                            rhs=words[:, g, :, :].rearrange("p i b -> p (i b)").bitcast(FP8X4),
                            rhs_scale=scales[:, g, :, :].rearrange("p i b -> p (i b)"),
                            start=(g == 0),
                            stop=(g == PASSES - 1),
                        )
                for j in range(PACK // PAIRS):
                    t = pair * (PACK // PAIRS) + j
                    nc.scalar.activation(
                        out=planes[:, h, t, :],
                        in_=acc[:, j, :],
                        func=SILU,
                        bias=b3_cols[:, PASSES * e + h, t : t + 1],
                        scale=1.0,
                    )

        def regroup_h3(e, h, rows):
            words = slice(PACK * rows.start, PACK * rows.stop)
            nc.vector.tensor_copy(
                out=h3_grouped_tiles[e][:, h, words].rearrange("p (c j t) -> p c t j", j=4, t=PACK),
                in_=h3_plane_tiles[e][:, h, :, rows].rearrange("p t (c j) -> p c t j", j=4),
            )

        def regroup_h3_on_scalar(e, h, rows):
            words = slice(PACK * rows.start, PACK * rows.stop)
            nc.scalar.copy(
                out=h3_grouped_tiles[e][:, h, words].rearrange("p (b t) -> p b t", t=PACK),
                in_=h3_plane_tiles[e][:, h, :, rows].rearrange("p t b -> p b t"),
            )

        def stage2_pass(e, h, i, o):
            words, scales = h3_mx[e]
            nc.tensor.matmul_mx(
                out=o,
                lhsT=words[:, h, i, :].bitcast(FP8X4),
                lhsT_scale=scales[:, h, i, :],
                rhs=w4_sb[:, PASSES * e + h, :].bitcast(FP8X4),
                rhs_scale=w4_planes[:, PASSES * e + h, :],
                start=(h == 0),
                stop=(h == PASSES - 1),
            )

        def stage2(first, envs, pool, tag):
            o = pool.tile([P, HALVES, envs, D], F32, tag=tag)
            for e in range(envs):
                for i in range(HALVES):
                    for h in range(PASSES):
                        stage2_pass(first + e, h, i, o[:, i, e, :])
            return o

        def add_b4(o, first, envs):
            part = slice(first, first + envs)
            nc.vector.tensor_tensor(
                out=out_sb[:, :, part, :],
                in0=o[:],
                in1=b4_all[:, part, :].unsqueeze(1).to_broadcast([P, HALVES, envs, D]),
                op=ADD,
            )

        def store(first, envs):
            part = slice(first, first + envs)
            nc.sync.dma_start(out=out_by_env[:, :, part, :], in_=out_sb[:, :, part, :])

        def keep_clock(n):
            idle = psum_o.tile([P, BANK], F32, tag="o")
            for c in range(n):
                nc.tensor.matmul(
                    out=idle[:], lhsT=ones[:], rhs=b4_row[:, 0:BANK], start=True, stop=True
                )

        x_grouped = work.tile([P, PASSES, HALVES * P * PACK], BF16, align_bytes=64, tag="x_grouped")
        x_grouped_tiles[0] = x_grouped
        for i in range(HALVES):
            xt = psum_tr.tile([P, PASSES, PAIR_WORDS, P], F32, tag="tr")
            x_pairs = h2_tiles[0][:, i, :].bitcast(F32)
            for g in range(PASSES):
                for u in range(PAIR_WORDS):
                    nc.tensor.transpose(
                        out=xt[:, g, u, :],
                        in_=x_pairs[:, K_PASS // 2 * g + u : K_PASS // 2 * (g + 1) : PAIR_WORDS],
                        identity=ident[:],
                    )
            nc.scalar.copy(
                out=x_grouped[:, :, K_PASS * i : K_PASS * (i + 1)].bitcast(F32).rearrange("p g (b u) -> p g b u", b=P),
                in_=xt[:].rearrange("p g u b -> p g b u"),
            )

        b3_sorted = const.tile([P, PACK, P], F32)
        nc.vector.tensor_copy(out=b3_sorted[:], in_=b3_rows[:].rearrange("r (p t) -> r t p", t=PACK))
        b3_t = psum_o.tile([P, PACK, P], F32, tag="o")
        for t in range(PACK):
            nc.tensor.transpose(out=b3_t[:, t, :], in_=b3_sorted[:, t, :], identity=ident[:])
        b3_cols = const.tile([P, E * PASSES, PACK], F32)
        nc.scalar.copy(out=b3_cols[:], in_=b3_t[:, :, 0 : E * PASSES].rearrange("p t r -> p r t"))
        x_mx[0] = mx_tiles("x")
        for g in range(PASSES):
            quantise_half(x_grouped, x_mx[0], g, 0)
        permute_w3_planes(0)
        permute_w3(0, 0, slice(0, P))
        permute_w3(0, 1, slice(0, P))
        for g in range(PASSES):
            quantise_half(x_grouped, x_mx[0], g, 1)
        permute_w3(0, 0, slice(P, 2 * P))
        permute_w3(0, 1, slice(P, 2 * P))

        b4_all = const.tile([P, E, D], F32)
        for c in range(E * D // BANK):
            b4_bank = psum_o.tile([P, BANK], F32, tag="o")
            cols = slice(BANK * c, BANK * (c + 1))
            nc.tensor.matmul(out=b4_bank[:], lhsT=ones[:], rhs=b4_row[:, cols], start=True, stop=True)
            nc.scalar.copy(out=b4_all[:].rearrange("p e d -> p (e d)")[:, cols], in_=b4_bank[:])

        whole = slice(0, PASSES)
        lower_w3_planes(0)
        load_w3_pass(2, 0)
        load_h2(3, 1)
        load_w3_pass(2, 1)
        load_w3_pass(3, 0)
        load_h2(4, 1)
        load_w3_pass(3, 1)
        load_w3_planes(1)
        load_w3_pass(4, 0)
        load_h2(5, 1)
        load_w3_pass(4, 1)
        load_w3_pass(5, 0)
        load_h2(6, 1)
        load_w3_pass(5, 1)
        load_h2(7, 1)
        load_w3_pass(6, 0)
        load_w3_pass(6, 1)

        SH = 208
        def perm_step(e):
            pieces = PASSES if e == E - 1 else 1
            width = H // PACK // pieces
            for n in range(pieces):
                for g in range(PASSES):
                    permute_w3(e, g, slice(width * n, width * (n + 1)))
        def qx_step(e):
            x_mx[e] = mx_tiles("x")
            quantise(x_grouped_tiles[e], x_mx[e], whole)
        def tx(e):
            for g in range(PASSES):
                transpose_x(e, g, nc.scalar.copy)
        T2 = "pre"
        for e in range(E):
            if e == 1 and T2 == "pre":
                tx(2)
            stage1(e, 0)
            if e == 0:
                tx(1)
            if e == 1 and T2 == "mid":
                tx(2)
            if e == 1 and T2 == "half":
                transpose_x(2, 0, nc.scalar.copy)
            stage1(e, 1)
            if e == 1 and T2 == "half":
                transpose_x(2, 1, nc.scalar.copy)
            if e == 1 and T2 == "post":
                tx(2)
            if e + 1 < E:
                if SH < B:
                    regroup_h3_on_scalar(e, 0, slice(SH, B))
                if e == 0:
                    regroup_h3(e, 0, slice(0, SH))
                if e == 3:
                    permute_w3_planes(1)
                    lower_w3_planes(1)
                    load_w3(7, pieces=PASSES)
                    load_w4_planes()
                    load_w4(0 * PASSES, 2 * PASSES)
                    load_w4(2 * PASSES, 2 * PASSES)
                    load_w4(4 * PASSES, 2 * PASSES)
                    load_w4(6 * PASSES, 2 * PASSES)

                if e + 1 in (1, 2, 3, 4, 5, 6):
                    permute_w3(e + 1, 0, slice(0, H // PACK))
                    qx_step(e + 1)
                    permute_w3(e + 1, 1, slice(0, H // PACK))
                elif e + 1 >= 9:
                    perm_step(e + 1)
                    qx_step(e + 1)
                else:
                    qx_step(e + 1)
                    perm_step(e + 1)
                if e > 0:
                    regroup_h3(e, 0, slice(0, SH))
                regroup_h3(e, 1, slice(0, B))
                for h in range(PASSES):
                    quantise(h3_grouped_tiles[e], h3_mx[e], slice(h, h + 1))
            if 0 < e and e + 2 < E:
                tx(e + 2)

        e = E - 1
        o01 = stage2(0, 2, psum_o, "o")
        o23 = stage2(2, 2, psum_o, "o")
        o45 = stage2(4, 2, psum_mx, "mx")
        o6 = stage2(6, 1, psum_mx, "mx")
        regroup_h3(e, 0, slice(0, B))
        add_b4(o01, 0, 2)
        store(0, 2)
        add_b4(o23, 2, 2)
        store(2, 2)
        quantise(h3_grouped_tiles[e], h3_mx[e], slice(0, 1))
        add_b4(o45, 4, 2)
        store(4, 2)
        for i in range(HALVES):
            regroup_h3_on_scalar(e, 1, slice(P * i, P * (i + 1)))
        o_halves = []
        for i in range(HALVES):
            o_half = psum_tr.tile([P, D], F32, tag="tr")
            o_halves.append(o_half)
            stage2_pass(e, 0, i, o_half[:])
        for i in range(HALVES):
            quantise_half(h3_grouped_tiles[e], h3_mx[e], 1, i)
            stage2_pass(e, 1, i, o_halves[i][:])
        add_b4(o6, 6, 1)
        store(6, 1)
        for i in range(HALVES):
            nc.vector.tensor_tensor(
                out=out_sb[:, i, e, :], in0=o_halves[i][:], in1=b4_all[:, e, :], op=ADD
            )
            nc.sync.dma_start(out=out_by_env[:, i, e, :], in_=out_sb[:, i, e, :])
